import numpy as np
import ml_dtypes


def mxq(x, axis, fmt="e4m3"):
    dtype, down = {"e4m3": (ml_dtypes.float8_e4m3fn, 7), "e5m2": (ml_dtypes.float8_e5m2, 14)}[fmt]
    v = np.moveaxis(np.asarray(x, np.float32).astype(ml_dtypes.bfloat16).astype(np.float64), axis, -1)
    blocks = v.reshape(v.shape[:-1] + (-1, 32))
    amax = np.abs(blocks).max(-1, keepdims=True)
    byte = np.maximum(np.where(amax > 0, np.frexp(amax)[1] - 1 + 127, 0) - down, 1)
    scale = np.exp2(byte - 127.0)
    codes = (blocks / scale).astype(np.float32).astype(dtype).astype(np.float64)
    return np.moveaxis((codes * scale).reshape(v.shape), -1, axis)


WIDE = False


def mx_kscale(k):
    if not WIDE:
        return np.ones(k)
    levels = np.array([10, -10, 5, -5, 0])
    a = np.random.permutation(np.resize(levels, k // 512 * 4)).reshape(k // 512, 4)
    idx = np.arange(k)
    return np.exp2(a[idx // 512, idx % 128 // 32])


BF16 = ml_dtypes.bfloat16


def bf(x):
    return np.asarray(x, np.float32).astype(BF16)


def f64(x):
    return np.asarray(x).astype(np.float64)


E2M1 = np.array([0.0, 0.5, 1.0, 1.5, 2.0, 3.0, 4.0, 6.0, -0.0, -0.5, -1.0, -1.5, -2.0, -3.0, -4.0, -6.0])


def pack_weight(w, fmt):
    k, n = w.shape
    w = f64(bf(w)).reshape(k // 32, 32, n)
    amax = np.abs(w).max(1)
    if fmt == "e4m3":
        byte = np.frexp(amax)[1] - 1 + 127 - 7
    else:
        mant, ex = np.frexp(amax / 6.0)
        byte = np.where(mant > 0.5, ex, ex - 1) + 127
    byte = np.clip(np.where(amax > 0, byte, 1), 1, 254)
    scaled = (w * np.exp2(127.0 - byte)[:, None, :]).reshape(k, n).astype(np.float32)
    by_word = np.ascontiguousarray(scaled.reshape(k // 512, 128, 4, n).transpose(0, 1, 3, 2))
    if fmt == "e4m3":
        words = by_word.astype(ml_dtypes.float8_e4m3fn).view(np.uint8)
    else:
        c = by_word.astype(ml_dtypes.float4_e2m1fn).view(np.uint8) & 0xF
        words = c[..., 0::2] | (c[..., 1::2] << 4)
    return np.ascontiguousarray(words), np.ascontiguousarray(byte.astype(np.uint8).reshape(k // 512, 16, n))


def unpack_weight(words, scales, fmt):
    g, p, n, _ = words.shape
    if fmt == "e4m3":
        vals = np.ascontiguousarray(words).view(ml_dtypes.float8_e4m3fn).astype(np.float64)
    else:
        nib = np.empty((g, p, n, 4), np.uint8)
        nib[..., 0::2] = words & 0xF
        nib[..., 1::2] = words >> 4
        vals = E2M1[nib]
    vals = vals * np.repeat(np.exp2(scales.astype(np.float64) - 127.0), 8, axis=1)[..., None]
    return vals.transpose(0, 1, 3, 2).reshape(g * 512, n)


B, N, C = 16, 16, 1024
BN_EPS = 1e-5
FMT = "e4m3"


def bn(v):
    mean = v.mean(axis=(0, 2), keepdims=True)
    var = v.var(axis=(0, 2), keepdims=True)
    return (v - mean) / np.sqrt(var + BN_EPS)


def sigmoid(v):
    return 1.0 / (1.0 + np.exp(-v))


def softmax(v, axis):
    p = np.exp(v - v.max(axis=axis, keepdims=True))
    return p / p.sum(axis=axis, keepdims=True)


def draw_w(a, f):
    w = np.random.standard_normal((C, C)) * a / np.sqrt(C) / f[None, :]
    return pack_weight(np.ascontiguousarray(w.T), FMT)


def setup_inputs():
    s, t = mx_kscale(C), mx_kscale(C)
    s, t = s / s.max(), t / t.max()
    x = bf(np.random.standard_normal((B, N, C)) * s)
    edge = bf(np.random.standard_normal((B, N * N, C)) * t)
    WA_words, WA_scales = draw_w(np.sqrt(2.0), s)
    WB_words, WB_scales = draw_w(np.sqrt(2.0), s)
    WE_words, WE_scales = draw_w(np.sqrt(2.0), t)
    WU_words, WU_scales = draw_w(0.4, s)
    WV_words, WV_scales = draw_w(0.5 * N, s)
    return {"x": x,
            "edge": edge,
            "WA_words": WA_words, "WA_scales": WA_scales,
            "WB_words": WB_words, "WB_scales": WB_scales,
            "WE_words": WE_words, "WE_scales": WE_scales,
            "WU_words": WU_words, "WU_scales": WU_scales,
            "WV_words": WV_words, "WV_scales": WV_scales}


def reference(x, edge, WA_words, WA_scales, WB_words, WB_scales, WE_words, WE_scales, WU_words, WU_scales, WV_words, WV_scales):
    x, edge = f64(x), f64(edge)
    xq = mxq(x, 2, "e4m3")
    Vix = xq @ unpack_weight(WA_words, WA_scales, FMT)
    Vjx = xq @ unpack_weight(WB_words, WB_scales, FMT)
    e_proj = mxq(edge, 2, "e4m3") @ unpack_weight(WE_words, WE_scales, FMT)
    agg = np.repeat(Vix, N, axis=1) + np.tile(Vjx, (1, N, 1)) + e_proj
    edge_out = edge + np.maximum(bn(agg), 0.0)
    e = sigmoid(edge_out).reshape(B, N, N, C)
    e = softmax(e, 2).reshape(B, N * N, C)
    Ujx = np.tile(xq @ unpack_weight(WV_words, WV_scales, FMT), (1, N, 1))
    Uix = xq @ unpack_weight(WU_words, WU_scales, FMT)
    msg = (e * Ujx).reshape(B, N, N, C).sum(axis=2)
    x_new = Uix + msg / N
    x_out = np.maximum(x + bn(x_new), 0.0)
    return x_out, edge_out

@@ -1,0 +1,411 @@
+from contextlib import ExitStack
+
+import concourse.mybir as mybir
+from concourse.masks import make_identity
+
+F32 = mybir.dt.float32
+BF16 = mybir.dt.bfloat16
+I32 = mybir.dt.int32
+U32 = mybir.dt.uint32
+U8 = mybir.dt.uint8
+FP8X4 = mybir.dt.float8_e4m3fn_x4
+ACT = mybir.ActivationFunctionType
+ALU = mybir.AluOpType
+AX = mybir.AxisListType
+
+P = 128
+GRAPHS = 16
+NODES = 16
+C = 1024
+HALVES = 2
+IL = NODES // HALVES
+PACK = 4
+PASSES = C // (P * PACK)
+PAIRS = PACK // 2
+BANK = 512
+BANKS = C // BANK
+BN_EPS = 1e-5
+
+FLOPS = 2 * (GRAPHS * NODES * NODES + 4 * GRAPHS * NODES) * C * C
+
+
+def tile_graphmodel_pa_t_kernel(
+    tc,
+    x,
+    edge,
+    WA_words,
+    WA_scales,
+    WB_words,
+    WB_scales,
+    WE_words,
+    WE_scales,
+    WU_words,
+    WU_scales,
+    WV_words,
+    WV_scales,
+    out_0,
+    out_1,
+):
+    nc = tc.nc
+
+    x_rows = x.rearrange("b (h i) c -> h b i c", h=HALVES)
+    x_out_rows = out_0.rearrange("b (h i) c -> h b i c", h=HALVES)
+    edge_rows = edge.rearrange("b (h i j) c -> h j b i c", h=HALVES, i=IL)
+    edge_out_rows = out_1.rearrange("b (h i j) c -> h j b i c", h=HALVES, i=IL)
+
+    with ExitStack() as ctx:
+        keep = ctx.enter_context(tc.tile_pool(name="keep", bufs=1))
+        work = ctx.enter_context(tc.tile_pool(name="work", bufs=2))
+        small = ctx.enter_context(tc.tile_pool(name="small", bufs=3))
+        acc_psum = ctx.enter_context(tc.psum_pool(name="acc_psum", bufs=3))
+        send_psum = ctx.enter_context(tc.psum_pool(name="send_psum", bufs=2))
+        flip_psum = ctx.enter_context(tc.psum_pool(name="flip_psum", bufs=2))
+        stat_psum = ctx.enter_context(tc.psum_pool(name="stat_psum", bufs=1))
+        ctx.enter_context(tc.manual_schedule())
+
+        given = {
+            "WE": (WE_words, WE_scales),
+            "WA": (WA_words, WA_scales),
+            "WB": (WB_words, WB_scales),
+            "WV": (WV_words, WV_scales),
+            "WU": (WU_words, WU_scales),
+        }
+        names = ("WE", "WA", "WB", "WV", "WU")
+        plane_tiles = []
+        for t in range((len(names) + 1) // 2):
+            planes = keep.tile([P, C], U8, name="planes%d" % t, align_bytes=64)
+            nc.vector.memset(planes[:].bitcast(I32), 0)
+            plane_tiles.append(planes)
+        w_words = {}
+        w_plane = {}
+        for idx, name in enumerate(names):
+            w_words[name] = keep.tile([P, PASSES, C], U32, name="words_" + name, align_bytes=64)
+            for g in range(PASSES):
+                w_plane[(name, g)] = plane_tiles[idx // 2][PACK * (PASSES * (idx % 2) + g) : P, :]
+
+        def load_scales(name):
+            scales = given[name][1]
+            idx = names.index(name)
+            first = PACK * PASSES * (idx % 2)
+            for quad in range(4):
+                nc.sync.dma_start(
+                    out=plane_tiles[idx // 2][
+                        32 * quad + first : 32 * quad + first + PACK * PASSES, :
+                    ].bitcast(I32),
+                    in_=scales[:, 4 * quad : 4 * quad + 4, :].bitcast(I32),
+                )
+
+        def load_words(name):
+            nc.sync.dma_start(
+                out=w_words[name][:].bitcast(I32),
+                in_=given[name][0].rearrange("g p n t -> p g (n t)").bitcast(I32),
+            )
+
+        def mx_group(acc, terms, cols):
+            last = len(terms) * PASSES - 1
+            done = 0
+            for codes, scales, name in terms:
+                for g in range(PASSES):
+                    nc.tensor.matmul_mx(
+                        out=acc,
+                        lhsT=codes[:, g, :].bitcast(FP8X4),
+                        lhsT_scale=scales[:, g, :],
+                        rhs=w_words[name][:, g, cols].bitcast(FP8X4),
+                        rhs_scale=w_plane[(name, g)][:, cols],
+                        start=(done == 0),
+                        stop=(done == last),
+                    )
+                    done += 1
+
+        def as_words(grouped):
+            flat = grouped.rearrange("p g r t -> p (g r t)").bitcast(F32)
+            return flat.rearrange("p (g r u) -> p g r u", g=PASSES, u=PAIRS)
+
+        def features_to_partitions(rows, grouped):
+            words = rows.bitcast(F32)
+            flipped = flip_psum.tile([P, PASSES, PAIRS, P], F32, name="flipped")
+            for g in range(PASSES):
+                for u in range(PAIRS):
+                    nc.tensor.transpose(
+                        flipped[:, g, u, :],
+                        words[:, (C // 4) * g + u : (C // 4) * (g + 1) : PAIRS],
+                        ident[:],
+                    )
+            nc.scalar.copy(out=as_words(grouped), in_=flipped[:].rearrange("p g u r -> p g r u"))
+
+        def batch_norm(sums, squares):
+            moments = stat_psum.tile([P, HALVES * (BANKS + 1)], F32, name="moments")
+            nc.tensor.matmul(
+                out=moments[:, 0 : HALVES * BANKS],
+                lhsT=group_mean[:],
+                rhs=sums[:].rearrange("p h n -> p (h n)"),
+                start=True,
+                stop=True,
+            )
+            nc.tensor.matmul(
+                out=moments[:, HALVES * BANKS :],
+                lhsT=group_mean[:],
+                rhs=squares[:],
+                start=True,
+                stop=True,
+            )
+            mean = small.tile([P, HALVES], F32, name="mean")
+            nc.vector.tensor_reduce(
+                out=mean[:],
+                in_=moments[:, 0 : HALVES * BANKS].rearrange("p (h n) -> p h n", n=BANKS),
+                axis=AX.X,
+                op=ALU.add,
+            )
+            mean_sq = small.tile([P, HALVES], F32, name="mean_sq")
+            nc.vector.tensor_tensor(out=mean_sq[:], in0=mean[:], in1=mean[:], op=ALU.mult)
+            var_eps = small.tile([P, HALVES], F32, name="var_eps")
+            nc.vector.scalar_tensor_tensor(
+                out=var_eps[:],
+                in0=moments[:, HALVES * BANKS :],
+                scalar=BN_EPS,
+                in1=mean_sq[:],
+                op0=ALU.add,
+                op1=ALU.subtract,
+            )
+            rstd = small.tile([P, HALVES], F32, name="rstd")
+            nc.gpsimd.tensor_tensor(out=rstd[:], in0=var_eps[:], in1=minus_half[:], op=ALU.pow)
+            return mean, rstd
+
+        def sum_of_squares(values, squares_col):
+            unread = work.tile([P, C], BF16, name="unread")
+            nc.scalar.activation(out=unread[:], in_=values, func=ACT.Square, accum_out=squares_col)
+
+        x_sb = keep.tile([P, HALVES, C], BF16, name="x_sb")
+        for h in range(HALVES):
+            nc.sync.dma_start(out=x_sb[:, h, :], in_=x_rows[h])
+
+        edge_sb = {}
+
+        def load(j):
+            edge_sb[j] = work.tile([P, HALVES, C], BF16, name="edge_sb", bufs=5)
+            for h in range(HALVES):
+                nc.sync.dma_start(out=edge_sb[j][:, h, :], in_=edge_rows[h, j])
+
+        load(0)
+        for group in (names[:3], names[3:]):
+            for name in group:
+                load_scales(name)
+            for name in group:
+                load_words(name)
+
+        ident = keep.tile([P, P], F32, name="ident")
+        make_identity(nc, ident[:])
+        same_il = keep.tile([P, IL], F32, name="same_il")
+        nc.vector.tensor_reduce(
+            out=same_il[:], in_=ident[:].rearrange("p (b i) -> p i b", i=IL), axis=AX.X, op=ALU.add
+        )
+        group_mean = keep.tile([P, P], F32, name="group_mean")
+        nc.vector.tensor_scalar_mul(
+            out=group_mean[:].rearrange("p (b i) -> p b i", i=IL),
+            in0=same_il[:].unsqueeze(1).to_broadcast([P, GRAPHS, IL]),
+            scalar1=1.0 / (GRAPHS * C),
+        )
+        minus_half = keep.tile([P, HALVES], F32, name="minus_half")
+        nc.vector.memset(minus_half[:], -0.5)
+
+        x_grouped = keep.tile([P, HALVES, PASSES, P, PACK], BF16, name="x_grouped", align_bytes=64)
+        for h in range(HALVES):
+            features_to_partitions(x_sb[:, h, :], x_grouped[:, h])
+        x_codes = keep.tile([P, HALVES, PASSES, P], U32, name="x_codes", align_bytes=64)
+        x_scales = keep.tile([P, HALVES, PASSES, P], U8, name="x_scales", align_bytes=64)
+        nc.vector.quantize_mx(
+            out=x_codes[:].rearrange("p h g r -> p (h g r)").bitcast(FP8X4),
+            scales=x_scales[:].rearrange("p h g r -> p (h g r)"),
+            in_=x_grouped[:].rearrange("p h g r t -> p (h g r t)"),
+        )
+
+        sender_codes = keep.tile([P, HALVES, PASSES, IL, P], U32, name="sender_codes", align_bytes=64)
+        sender_scales = keep.tile([P, HALVES, PASSES, IL, P], U8, name="sender_scales", align_bytes=64)
+
+        def repeat_senders(h):
+            for g in range(PASSES):
+                repeated = work.tile([P, IL * P * PACK], BF16, name="repeated", bufs=1, align_bytes=64)
+                nc.vector.tensor_copy(
+                    out=repeated[:]
+                    .bitcast(F32)
+                    .rearrange("p (l b i u) -> p l b i u", l=IL, b=GRAPHS, i=IL),
+                    in_=as_words(x_grouped[:, h])[:, g]
+                    .rearrange("p (b l) u -> p l b u", l=IL)
+                    .unsqueeze(3)
+                    .to_broadcast([P, IL, GRAPHS, IL, PAIRS]),
+                )
+                nc.vector.quantize_mx(
+                    out=sender_codes[:, h, g].rearrange("p l r -> p (l r)").bitcast(FP8X4),
+                    scales=sender_scales[:, h, g].rearrange("p l r -> p (l r)"),
+                    in_=repeated[:],
+                )
+
+        def sender(j):
+            return sender_codes[:, j // IL, :, j % IL, :], sender_scales[:, j // IL, :, j % IL, :]
+
+        edge_codes = {}
+        edge_scales = {}
+        agg = {}
+        sums = {}
+        squares = {}
+        norm = {}
+        edge_out = {}
+        soft = {}
+        soft_sum = keep.tile([P, HALVES, C], F32, name="soft_sum")
+        gated_sum = keep.tile([P, HALVES, C], F32, name="gated_sum")
+
+        def prepare(j):
+            grouped = work.tile([P, HALVES, PASSES, P, PACK], BF16, name="grouped", align_bytes=64)
+            for h in range(HALVES):
+                features_to_partitions(edge_sb[j][:, h, :], grouped[:, h])
+            edge_codes[j] = work.tile([P, HALVES, PASSES, P], U32, name="edge_codes", bufs=3, align_bytes=64)
+            edge_scales[j] = work.tile([P, HALVES, PASSES, P], U8, name="edge_scales", bufs=3, align_bytes=64)
+            nc.vector.quantize_mx(
+                out=edge_codes[j][:].rearrange("p h g r -> p (h g r)").bitcast(FP8X4),
+                scales=edge_scales[j][:].rearrange("p h g r -> p (h g r)"),
+                in_=grouped[:].rearrange("p h g r t -> p (h g r t)"),
+            )
+
+        def project(j, h):
+            if h == 0:
+                agg[j] = work.tile([P, HALVES, C], F32, name="agg", bufs=3)
+                sums[j] = small.tile([P, HALVES, BANKS], F32, name="sums")
+                squares[j] = small.tile([P, HALVES], F32, name="squares")
+            send_codes, send_scales = sender(j)
+            for n in range(BANKS):
+                cols = slice(n * BANK, (n + 1) * BANK)
+                acc = acc_psum.tile([P, BANK], F32, name="acc")
+                mx_group(
+                    acc[:],
+                    (
+                        (edge_codes[j][:, h], edge_scales[j][:, h], "WE"),
+                        (x_codes[:, h], x_scales[:, h], "WA"),
+                        (send_codes, send_scales, "WB"),
+                    ),
+                    cols,
+                )
+                nc.scalar.activation(
+                    out=agg[j][:, h, cols], in_=acc[:], func=ACT.Identity, accum_out=sums[j][:, h, n : n + 1]
+                )
+            sum_of_squares(agg[j][:, h, :], squares[j][:, h : h + 1])
+
+        def norm_stats(j):
+            norm[j] = batch_norm(sums[j], squares[j])
+
+        def normalise(j):
+            mean, rstd = norm[j]
+            edge_out[j] = work.tile([P, HALVES, C], F32, name="edge_out")
+            for h in range(HALVES):
+                nc.vector.tensor_scalar(
+                    out=agg[j][:, h, :],
+                    in0=agg[j][:, h, :],
+                    scalar1=mean[:, h : h + 1],
+                    scalar2=0.0,
+                    op0=ALU.subtract,
+                    op1=ALU.max,
+                )
+            for h in range(HALVES):
+                nc.vector.scalar_tensor_tensor(
+                    out=edge_out[j][:, h, :],
+                    in0=agg[j][:, h, :],
+                    scalar=rstd[:, h : h + 1],
+                    in1=edge_sb[j][:, h, :],
+                    op0=ALU.mult,
+                    op1=ALU.add,
+                )
+                nc.sync.dma_start(out=edge_out_rows[h, j], in_=edge_out[j][:, h, :])
+
+        def squash(j):
+            soft[j] = soft_sum if j == 0 else work.tile([P, HALVES, C], F32, name="soft")
+            nc.scalar.activation(out=soft[j][:], in_=edge_out[j][:], func=ACT.Tanh, scale=0.5)
+
+        def exponentiate(j):
+            nc.scalar.activation(out=soft[j][:], in_=soft[j][:], func=ACT.Exp, scale=0.5)
+
+        def message(j):
+            gated = gated_sum if j == 0 else work.tile([P, HALVES, C], F32, name="gated", bufs=1)
+            send_codes, send_scales = sender(j)
+            for n in range(BANKS):
+                cols = slice(n * BANK, (n + 1) * BANK)
+                sent = send_psum.tile([P, BANK], F32, name="sent")
+                mx_group(sent[:], ((send_codes, send_scales, "WV"),), cols)
+                nc.vector.tensor_tensor(
+                    out=gated[:, :, cols],
+                    in0=soft[j][:, :, cols],
+                    in1=sent[:].unsqueeze(1).to_broadcast([P, HALVES, BANK]),
+                    op=ALU.mult,
+                )
+            if j > 0:
+                nc.vector.tensor_tensor(out=soft_sum[:], in0=soft_sum[:], in1=soft[j][:], op=ALU.add)
+                nc.vector.tensor_tensor(out=gated_sum[:], in0=gated_sum[:], in1=gated[:], op=ALU.add)
+
+        def due(j):
+            return 0 <= j < NODES
+
+        repeat_senders(0)
+        prepare(0)
+        load(1)
+        prepare(1)
+        load(2)
+        repeat_senders(1)
+        for r in range(NODES + 3):
+            if due(r):
+                project(r, 0)
+            if due(r - 1):
+                norm_stats(r - 1)
+            if due(r - 3):
+                message(r - 3)
+            if due(r - 2):
+                squash(r - 2)
+            if due(r - 1):
+                normalise(r - 1)
+            if due(r):
+                project(r, 1)
+            if due(r - 2):
+                exponentiate(r - 2)
+            if due(r + 2):
+                prepare(r + 2)
+            if due(r + 3):
+                load(r + 3)
+
+        inverse = work.tile([P, HALVES, C], F32, name="inverse", tag="soft")
+        nc.scalar.activation(out=inverse[:], in_=soft_sum[:], func=ACT.Abs_reciprocal_sqrt)
+        nc.scalar.activation(out=inverse[:], in_=inverse[:], func=ACT.Square, scale=0.25)
+        nc.vector.tensor_tensor(out=gated_sum[:], in0=gated_sum[:], in1=inverse[:], op=ALU.mult)
+        x_new = work.tile([P, HALVES, C], F32, name="x_new", tag="agg", bufs=3)
+        x_sums = small.tile([P, HALVES, BANKS], F32, name="x_sums")
+        x_squares = small.tile([P, HALVES], F32, name="x_squares")
+        for h in range(HALVES):
+            for n in range(BANKS):
+                cols = slice(n * BANK, (n + 1) * BANK)
+                acc = acc_psum.tile([P, BANK], F32, name="acc")
+                mx_group(acc[:], ((x_codes[:, h], x_scales[:, h], "WU"),), cols)
+                nc.vector.scalar_tensor_tensor(
+                    out=x_new[:, h, cols],
+                    in0=gated_sum[:, h, cols],
+                    scalar=1.0,
+                    in1=acc[:],
+                    op0=ALU.mult,
+                    op1=ALU.add,
+                    accum_out=x_sums[:, h, n : n + 1],
+                )
+            sum_of_squares(x_new[:, h, :], x_squares[:, h : h + 1])
+        mean, rstd = batch_norm(x_sums, x_squares)
+        shift = small.tile([P, HALVES], F32, name="shift")
+        nc.vector.scalar_tensor_tensor(
+            out=shift[:], in0=mean[:], scalar=-1.0, in1=rstd[:], op0=ALU.mult, op1=ALU.mult
+        )
+        x_out = work.tile([P, HALVES, C], F32, name="x_out", tag="edge_out")
+        for h in range(HALVES):
+            nc.vector.scalar_tensor_tensor(
+                out=x_out[:, h, :],
+                in0=x_new[:, h, :],
+                scalar=rstd[:, h : h + 1],
+                in1=x_sb[:, h, :],
+                op0=ALU.mult,
+                op1=ALU.add,
+            )
+            nc.scalar.activation(
+                out=x_out[:, h, :], in_=x_out[:, h, :], func=ACT.Relu, bias=shift[:, h : h + 1]
+            )
+            nc.sync.dma_start(out=x_out_rows[h], in_=x_out[:, h, :])

@@ -25,6 +25,8 @@ PAIRS = PACK // 2
 BANK = 512
 BANKS = C // BANK
 BN_EPS = 1e-5
+QUANTISE_AHEAD = 2
+LOAD_AHEAD = 4
 
 FLOPS = 2 * (GRAPHS * NODES * NODES + 4 * GRAPHS * NODES) * C * C
 
@@ -70,29 +72,22 @@ def tile_graphmodel_pa_t_kernel(
             "WV": (WV_words, WV_scales),
             "WU": (WU_words, WU_scales),
         }
-        names = ("WE", "WA", "WB", "WV", "WU")
-        plane_tiles = []
-        for t in range((len(names) + 1) // 2):
-            planes = keep.tile([P, C], U8, name="planes%d" % t, align_bytes=64)
-            nc.vector.memset(planes[:].bitcast(I32), 0)
-            plane_tiles.append(planes)
+        sharing = (("WE", "WA"), ("WB",), ("WV", "WU"))
         w_words = {}
-        w_plane = {}
-        for idx, name in enumerate(names):
-            w_words[name] = keep.tile([P, PASSES, C], U32, name="words_" + name, align_bytes=64)
-            for g in range(PASSES):
-                w_plane[(name, g)] = plane_tiles[idx // 2][PACK * (PASSES * (idx % 2) + g) : P, :]
+        w_planes = {}
+        for names in sharing:
+            planes = keep.tile([P, C], U8, name="planes_" + names[0], align_bytes=64)
+            nc.vector.memset(planes[:].bitcast(I32), 0)
+            for place, name in enumerate(names):
+                w_planes[name] = (planes, PACK * PASSES * place)
+                w_words[name] = keep.tile([P, PASSES, C], U32, name="words_" + name, align_bytes=64)
 
         def load_scales(name):
-            scales = given[name][1]
-            idx = names.index(name)
-            first = PACK * PASSES * (idx % 2)
+            planes, first = w_planes[name]
             for quad in range(4):
                 nc.sync.dma_start(
-                    out=plane_tiles[idx // 2][
-                        32 * quad + first : 32 * quad + first + PACK * PASSES, :
-                    ].bitcast(I32),
-                    in_=scales[:, 4 * quad : 4 * quad + 4, :].bitcast(I32),
+                    out=planes[32 * quad + first : 32 * quad + first + PACK * PASSES, :].bitcast(I32),
+                    in_=given[name][1][:, 4 * quad : 4 * quad + 4, :].bitcast(I32),
                 )
 
         def load_words(name):
@@ -105,13 +100,14 @@ def tile_graphmodel_pa_t_kernel(
             last = len(terms) * PASSES - 1
             done = 0
             for codes, scales, name in terms:
+                planes, first = w_planes[name]
                 for g in range(PASSES):
                     nc.tensor.matmul_mx(
                         out=acc,
                         lhsT=codes[:, g, :].bitcast(FP8X4),
                         lhsT_scale=scales[:, g, :],
                         rhs=w_words[name][:, g, cols].bitcast(FP8X4),
-                        rhs_scale=w_plane[(name, g)][:, cols],
+                        rhs_scale=planes[first + PACK * g : P, cols],
                         start=(done == 0),
                         stop=(done == last),
                     )
@@ -182,16 +178,23 @@ def tile_graphmodel_pa_t_kernel(
         edge_sb = {}
 
         def load(j):
-            edge_sb[j] = work.tile([P, HALVES, C], BF16, name="edge_sb", bufs=5)
+            edge_sb[j] = work.tile([P, HALVES, C], BF16, name="edge_sb", bufs=LOAD_AHEAD + 1)
             for h in range(HALVES):
                 nc.sync.dma_start(out=edge_sb[j][:, h, :], in_=edge_rows[h, j])
 
         load(0)
-        for group in (names[:3], names[3:]):
-            for name in group:
-                load_scales(name)
-            for name in group:
-                load_words(name)
+        load(1)
+        for name in ("WE", "WA", "WB"):
+            load_scales(name)
+        for name in ("WE", "WA", "WB"):
+            load_words(name)
+        load(2)
+        for name in ("WV", "WU"):
+            load_scales(name)
+        for name in ("WV", "WU"):
+            load_words(name)
+        load(3)
+        assert LOAD_AHEAD == 4
 
         ident = keep.tile([P, P], F32, name="ident")
         make_identity(nc, ident[:])
@@ -243,6 +246,7 @@ def tile_graphmodel_pa_t_kernel(
         def sender(j):
             return sender_codes[:, j // IL, :, j % IL, :], sender_scales[:, j // IL, :, j % IL, :]
 
+        grouped = {}
         edge_codes = {}
         edge_scales = {}
         agg = {}
@@ -254,16 +258,18 @@ def tile_graphmodel_pa_t_kernel(
         soft_sum = keep.tile([P, HALVES, C], F32, name="soft_sum")
         gated_sum = keep.tile([P, HALVES, C], F32, name="gated_sum")
 
-        def prepare(j):
-            grouped = work.tile([P, HALVES, PASSES, P, PACK], BF16, name="grouped", align_bytes=64)
+        def flip(j):
+            grouped[j] = work.tile([P, HALVES, PASSES, P, PACK], BF16, name="grouped", align_bytes=64)
             for h in range(HALVES):
-                features_to_partitions(edge_sb[j][:, h, :], grouped[:, h])
+                features_to_partitions(edge_sb[j][:, h, :], grouped[j][:, h])
+
+        def quantise(j):
             edge_codes[j] = work.tile([P, HALVES, PASSES, P], U32, name="edge_codes", bufs=3, align_bytes=64)
             edge_scales[j] = work.tile([P, HALVES, PASSES, P], U8, name="edge_scales", bufs=3, align_bytes=64)
             nc.vector.quantize_mx(
                 out=edge_codes[j][:].rearrange("p h g r -> p (h g r)").bitcast(FP8X4),
                 scales=edge_scales[j][:].rearrange("p h g r -> p (h g r)"),
-                in_=grouped[:].rearrange("p h g r t -> p (h g r t)"),
+                in_=grouped[j][:].rearrange("p h g r t -> p (h g r t)"),
             )
 
         def project(j, h):
@@ -322,7 +328,11 @@ def tile_graphmodel_pa_t_kernel(
         def exponentiate(j):
             nc.scalar.activation(out=soft[j][:], in_=soft[j][:], func=ACT.Exp, scale=0.5)
 
-        def message(j):
+        def add_soft(j):
+            if j > 0:
+                nc.vector.tensor_tensor(out=soft_sum[:], in0=soft_sum[:], in1=soft[j][:], op=ALU.add)
+
+        def add_gated(j):
             gated = gated_sum if j == 0 else work.tile([P, HALVES, C], F32, name="gated", bufs=1)
             send_codes, send_scales = sender(j)
             for n in range(BANKS):
@@ -336,46 +346,54 @@ def tile_graphmodel_pa_t_kernel(
                     op=ALU.mult,
                 )
             if j > 0:
-                nc.vector.tensor_tensor(out=soft_sum[:], in0=soft_sum[:], in1=soft[j][:], op=ALU.add)
-                nc.vector.tensor_tensor(out=gated_sum[:], in0=gated_sum[:], in1=gated[:], op=ALU.add)
+                for n in range(BANKS):
+                    cols = slice(n * BANK, (n + 1) * BANK)
+                    nc.vector.tensor_tensor(
+                        out=gated_sum[:, :, cols], in0=gated_sum[:, :, cols], in1=gated[:, :, cols], op=ALU.add
+                    )
 
         def due(j):
             return 0 <= j < NODES
 
         repeat_senders(0)
-        prepare(0)
-        load(1)
-        prepare(1)
-        load(2)
+        for j in range(QUANTISE_AHEAD):
+            flip(j)
+            quantise(j)
         repeat_senders(1)
-        for r in range(NODES + 3):
-            if due(r):
-                project(r, 0)
-            if due(r - 1):
-                norm_stats(r - 1)
-            if due(r - 3):
-                message(r - 3)
+        for r in range(NODES + 2):
             if due(r - 2):
                 squash(r - 2)
+                exponentiate(r - 2)
+            if due(r):
+                project(r, 0)
             if due(r - 1):
                 normalise(r - 1)
             if due(r):
                 project(r, 1)
+            if due(r + QUANTISE_AHEAD):
+                flip(r + QUANTISE_AHEAD)
             if due(r - 2):
-                exponentiate(r - 2)
-            if due(r + 2):
-                prepare(r + 2)
-            if due(r + 3):
-                load(r + 3)
+                add_soft(r - 2)
+            if due(r):
+                norm_stats(r)
+            if due(r - 2):
+                add_gated(r - 2)
+            if due(r + QUANTISE_AHEAD):
+                quantise(r + QUANTISE_AHEAD)
+            if due(r + LOAD_AHEAD):
+                load(r + LOAD_AHEAD)
 
         inverse = work.tile([P, HALVES, C], F32, name="inverse", tag="soft")
-        nc.scalar.activation(out=inverse[:], in_=soft_sum[:], func=ACT.Abs_reciprocal_sqrt)
-        nc.scalar.activation(out=inverse[:], in_=inverse[:], func=ACT.Square, scale=0.25)
-        nc.vector.tensor_tensor(out=gated_sum[:], in0=gated_sum[:], in1=inverse[:], op=ALU.mult)
+        for h in range(HALVES):
+            nc.scalar.activation(out=inverse[:, h, :], in_=soft_sum[:, h, :], func=ACT.Abs_reciprocal_sqrt)
+            nc.scalar.activation(out=inverse[:, h, :], in_=inverse[:, h, :], func=ACT.Square, scale=0.25)
         x_new = work.tile([P, HALVES, C], F32, name="x_new", tag="agg", bufs=3)
         x_sums = small.tile([P, HALVES, BANKS], F32, name="x_sums")
         x_squares = small.tile([P, HALVES], F32, name="x_squares")
         for h in range(HALVES):
+            nc.vector.tensor_tensor(
+                out=gated_sum[:, h, :], in0=gated_sum[:, h, :], in1=inverse[:, h, :], op=ALU.mult
+            )
             for n in range(BANKS):
                 cols = slice(n * BANK, (n + 1) * BANK)
                 acc = acc_psum.tile([P, BANK], F32, name="acc")

@@ -63,7 +63,6 @@ def tile_graphmodel_pa_t_kernel(
         send_psum = ctx.enter_context(tc.psum_pool(name="send_psum", bufs=2))
         flip_psum = ctx.enter_context(tc.psum_pool(name="flip_psum", bufs=2))
         stat_psum = ctx.enter_context(tc.psum_pool(name="stat_psum", bufs=1))
-        ctx.enter_context(tc.manual_schedule())
 
         given = {
             "WE": (WE_words, WE_scales),
@@ -255,6 +254,7 @@ def tile_graphmodel_pa_t_kernel(
         norm = {}
         edge_out = {}
         soft = {}
+        sent = {}
         soft_sum = keep.tile([P, HALVES, C], F32, name="soft_sum")
         gated_sum = keep.tile([P, HALVES, C], F32, name="gated_sum")
 
@@ -332,17 +332,22 @@ def tile_graphmodel_pa_t_kernel(
             if j > 0:
                 nc.vector.tensor_tensor(out=soft_sum[:], in0=soft_sum[:], in1=soft[j][:], op=ALU.add)
 
+        def send(j):
+            send_codes, send_scales = sender(j)
+            sent[j] = []
+            for n in range(BANKS):
+                bank = send_psum.tile([P, BANK], F32, name="sent")
+                mx_group(bank[:], ((send_codes, send_scales, "WV"),), slice(n * BANK, (n + 1) * BANK))
+                sent[j].append(bank)
+
         def add_gated(j):
             gated = gated_sum if j == 0 else work.tile([P, HALVES, C], F32, name="gated", bufs=1)
-            send_codes, send_scales = sender(j)
             for n in range(BANKS):
                 cols = slice(n * BANK, (n + 1) * BANK)
-                sent = send_psum.tile([P, BANK], F32, name="sent")
-                mx_group(sent[:], ((send_codes, send_scales, "WV"),), cols)
                 nc.vector.tensor_tensor(
                     out=gated[:, :, cols],
                     in0=soft[j][:, :, cols],
-                    in1=sent[:].unsqueeze(1).to_broadcast([P, HALVES, BANK]),
+                    in1=sent[j][n][:].unsqueeze(1).to_broadcast([P, HALVES, BANK]),
                     op=ALU.mult,
                 )
             if j > 0:
@@ -373,6 +378,7 @@ def tile_graphmodel_pa_t_kernel(
             if due(r + QUANTISE_AHEAD):
                 flip(r + QUANTISE_AHEAD)
             if due(r - 2):
+                send(r - 2)
                 add_soft(r - 2)
             if due(r):
                 norm_stats(r)

@@ -381,7 +381,8 @@ def tile_graphmodel_pa_t_kernel(
                 send(r - 2)
                 add_soft(r - 2)
             if due(r):
-                norm_stats(r)
+                with tc.high_priority():
+                    norm_stats(r)
             if due(r - 2):
                 add_gated(r - 2)
             if due(r + QUANTISE_AHEAD):

@@ -25,8 +25,14 @@ PAIRS = PACK // 2
 BANK = 512
 BANKS = C // BANK
 BN_EPS = 1e-5
-QUANTISE_AHEAD = 2
+BLOCKS = BANK // P
+TILES = HALVES * NODES
 LOAD_AHEAD = 4
+SENDERS = 4
+SOFT_BUFS = 3
+AGG_BUFS = 5
+
+LASTING = ("WE", "WB")
 
 FLOPS = 2 * (GRAPHS * NODES * NODES + 4 * GRAPHS * NODES) * C * C
 
@@ -59,10 +65,11 @@ def tile_graphmodel_pa_t_kernel(
         keep = ctx.enter_context(tc.tile_pool(name="keep", bufs=1))
         work = ctx.enter_context(tc.tile_pool(name="work", bufs=2))
         small = ctx.enter_context(tc.tile_pool(name="small", bufs=3))
-        acc_psum = ctx.enter_context(tc.psum_pool(name="acc_psum", bufs=3))
-        send_psum = ctx.enter_context(tc.psum_pool(name="send_psum", bufs=2))
-        flip_psum = ctx.enter_context(tc.psum_pool(name="flip_psum", bufs=2))
+        rows_pool = ctx.enter_context(tc.tile_pool(name="rows_pool", bufs=NODES))
+        acc_psum = ctx.enter_context(tc.psum_pool(name="acc_psum", bufs=2))
+        flip_psum = ctx.enter_context(tc.psum_pool(name="flip_psum", bufs=1))
         stat_psum = ctx.enter_context(tc.psum_pool(name="stat_psum", bufs=1))
+        sum_psum = ctx.enter_context(tc.psum_pool(name="sum_psum", bufs=2))
 
         given = {
             "WE": (WE_words, WE_scales),
@@ -79,7 +86,6 @@ def tile_graphmodel_pa_t_kernel(
             nc.vector.memset(planes[:].bitcast(I32), 0)
             for place, name in enumerate(names):
                 w_planes[name] = (planes, PACK * PASSES * place)
-                w_words[name] = keep.tile([P, PASSES, C], U32, name="words_" + name, align_bytes=64)
 
         def load_scales(name):
             planes, first = w_planes[name]
@@ -89,13 +95,20 @@ def tile_graphmodel_pa_t_kernel(
                     in_=given[name][1][:, 4 * quad : 4 * quad + 4, :].bitcast(I32),
                 )
 
-        def load_words(name):
+        def load_words(name, n):
+            if name in LASTING:
+                words = keep.tile([P, PASSES, BANK], U32, name="words_%s_%d" % (name, n), align_bytes=64)
+            else:
+                words = rows_pool.tile([P, PASSES, BANK], U32, name="words", tag="node_rows", align_bytes=64)
             nc.sync.dma_start(
-                out=w_words[name][:].bitcast(I32),
-                in_=given[name][0].rearrange("g p n t -> p g (n t)").bitcast(I32),
+                out=words[:].bitcast(I32),
+                in_=given[name][0][:, :, n * BANK : (n + 1) * BANK, :]
+                .rearrange("g p n t -> p g (n t)")
+                .bitcast(I32),
             )
+            w_words[name, n] = words
 
-        def mx_group(acc, terms, cols):
+        def mx_group(acc, terms, n):
             last = len(terms) * PASSES - 1
             done = 0
             for codes, scales, name in terms:
@@ -105,8 +118,8 @@ def tile_graphmodel_pa_t_kernel(
                         out=acc,
                         lhsT=codes[:, g, :].bitcast(FP8X4),
                         lhsT_scale=scales[:, g, :],
-                        rhs=w_words[name][:, g, cols].bitcast(FP8X4),
-                        rhs_scale=planes[first + PACK * g : P, cols],
+                        rhs=w_words[name, n][:, g, :].bitcast(FP8X4),
+                        rhs_scale=planes[first + PACK * g : P, n * BANK : (n + 1) * BANK],
                         start=(done == 0),
                         stop=(done == last),
                     )
@@ -128,46 +141,34 @@ def tile_graphmodel_pa_t_kernel(
                     )
             nc.scalar.copy(out=as_words(grouped), in_=flipped[:].rearrange("p g u r -> p g r u"))
 
-        def batch_norm(sums, squares):
-            moments = stat_psum.tile([P, HALVES * (BANKS + 1)], F32, name="moments")
-            nc.tensor.matmul(
-                out=moments[:, 0 : HALVES * BANKS],
-                lhsT=group_mean[:],
-                rhs=sums[:].rearrange("p h n -> p (h n)"),
-                start=True,
-                stop=True,
-            )
-            nc.tensor.matmul(
-                out=moments[:, HALVES * BANKS :],
-                lhsT=group_mean[:],
-                rhs=squares[:],
-                start=True,
-                stop=True,
-            )
-            mean = small.tile([P, HALVES], F32, name="mean")
-            nc.vector.tensor_reduce(
-                out=mean[:],
-                in_=moments[:, 0 : HALVES * BANKS].rearrange("p (h n) -> p h n", n=BANKS),
-                axis=AX.X,
-                op=ALU.add,
-            )
-            mean_sq = small.tile([P, HALVES], F32, name="mean_sq")
-            nc.vector.tensor_tensor(out=mean_sq[:], in0=mean[:], in1=mean[:], op=ALU.mult)
-            var_eps = small.tile([P, HALVES], F32, name="var_eps")
+        def moments_of(sums):
+            moments = stat_psum.tile([P, 2], F32, name="moments")
+            for n in range(BANKS):
+                nc.tensor.matmul(
+                    out=moments[:], lhsT=group_mean[:], rhs=sums[:, n, :], start=(n == 0), stop=(n == BANKS - 1)
+                )
+            mean = small.tile([P, 1], F32, name="mean")
+            nc.scalar.activation(out=mean[:], in_=moments[:, 0:1], func=ACT.Identity)
+            mean_sq = small.tile([P, 1], F32, name="mean_sq")
+            nc.scalar.activation(out=mean_sq[:], in_=moments[:, 0:1], func=ACT.Square)
+            return moments, mean, mean_sq
+
+        def inverse_deviation(moments, mean_sq):
+            var_eps = small.tile([P, 1], F32, name="var_eps")
             nc.vector.scalar_tensor_tensor(
                 out=var_eps[:],
-                in0=moments[:, HALVES * BANKS :],
+                in0=moments[:, 1:2],
                 scalar=BN_EPS,
                 in1=mean_sq[:],
                 op0=ALU.add,
                 op1=ALU.subtract,
             )
-            rstd = small.tile([P, HALVES], F32, name="rstd")
+            rstd = small.tile([P, 1], F32, name="rstd")
             nc.gpsimd.tensor_tensor(out=rstd[:], in0=var_eps[:], in1=minus_half[:], op=ALU.pow)
-            return mean, rstd
+            return rstd
 
         def sum_of_squares(values, squares_col):
-            unread = work.tile([P, C], BF16, name="unread")
+            unread = work.tile([P, BANK], BF16, name="unread")
             nc.scalar.activation(out=unread[:], in_=values, func=ACT.Square, accum_out=squares_col)
 
         x_sb = keep.tile([P, HALVES, C], BF16, name="x_sb")
@@ -176,24 +177,25 @@ def tile_graphmodel_pa_t_kernel(
 
         edge_sb = {}
 
-        def load(j):
-            edge_sb[j] = work.tile([P, HALVES, C], BF16, name="edge_sb", bufs=LOAD_AHEAD + 1)
-            for h in range(HALVES):
-                nc.sync.dma_start(out=edge_sb[j][:, h, :], in_=edge_rows[h, j])
+        def load(t):
+            h, j = divmod(t, NODES)
+            edge_sb[t] = work.tile([P, C], BF16, name="edge_sb", bufs=LOAD_AHEAD + 2)
+            nc.sync.dma_start(out=edge_sb[t][:], in_=edge_rows[h, j])
 
         load(0)
+        for name in ("WE", "WA", "WB"):
+            load_scales(name)
+        load_words("WE", 0)
         load(1)
-        for name in ("WE", "WA", "WB"):
-            load_scales(name)
-        for name in ("WE", "WA", "WB"):
-            load_words(name)
-        load(2)
+        for name, n in (("WA", 0), ("WB", 0), ("WE", 1), ("WA", 1), ("WB", 1)):
+            load_words(name, n)
+        for t in range(2, LOAD_AHEAD):
+            load(t)
         for name in ("WV", "WU"):
             load_scales(name)
         for name in ("WV", "WU"):
-            load_words(name)
-        load(3)
-        assert LOAD_AHEAD == 4
+            for n in range(BANKS):
+                load_words(name, n)
 
         ident = keep.tile([P, P], F32, name="ident")
         make_identity(nc, ident[:])
@@ -207,230 +209,318 @@ def tile_graphmodel_pa_t_kernel(
             in0=same_il[:].unsqueeze(1).to_broadcast([P, GRAPHS, IL]),
             scalar1=1.0 / (GRAPHS * C),
         )
-        minus_half = keep.tile([P, HALVES], F32, name="minus_half")
+        minus_half = keep.tile([P, 1], F32, name="minus_half")
         nc.vector.memset(minus_half[:], -0.5)
 
         x_grouped = keep.tile([P, HALVES, PASSES, P, PACK], BF16, name="x_grouped", align_bytes=64)
-        for h in range(HALVES):
-            features_to_partitions(x_sb[:, h, :], x_grouped[:, h])
         x_codes = keep.tile([P, HALVES, PASSES, P], U32, name="x_codes", align_bytes=64)
         x_scales = keep.tile([P, HALVES, PASSES, P], U8, name="x_scales", align_bytes=64)
-        nc.vector.quantize_mx(
-            out=x_codes[:].rearrange("p h g r -> p (h g r)").bitcast(FP8X4),
-            scales=x_scales[:].rearrange("p h g r -> p (h g r)"),
-            in_=x_grouped[:].rearrange("p h g r t -> p (h g r t)"),
-        )
+
+        def quantise_nodes():
+            nc.vector.quantize_mx(
+                out=x_codes[:].rearrange("p h g r -> p (h g r)").bitcast(FP8X4),
+                scales=x_scales[:].rearrange("p h g r -> p (h g r)"),
+                in_=x_grouped[:].rearrange("p h g r t -> p (h g r t)"),
+            )
 
         sender_codes = keep.tile([P, HALVES, PASSES, IL, P], U32, name="sender_codes", align_bytes=64)
         sender_scales = keep.tile([P, HALVES, PASSES, IL, P], U8, name="sender_scales", align_bytes=64)
 
-        def repeat_senders(h):
+        def repeat_senders(first):
+            h, l = divmod(first, IL)
+            group = slice(l, l + SENDERS)
             for g in range(PASSES):
-                repeated = work.tile([P, IL * P * PACK], BF16, name="repeated", bufs=1, align_bytes=64)
+                repeated = work.tile([P, SENDERS * P * PACK], BF16, name="repeated", align_bytes=64)
                 nc.vector.tensor_copy(
                     out=repeated[:]
                     .bitcast(F32)
-                    .rearrange("p (l b i u) -> p l b i u", l=IL, b=GRAPHS, i=IL),
+                    .rearrange("p (l b i u) -> p l b i u", l=SENDERS, b=GRAPHS, i=IL),
                     in_=as_words(x_grouped[:, h])[:, g]
-                    .rearrange("p (b l) u -> p l b u", l=IL)
+                    .rearrange("p (b l) u -> p l b u", l=IL)[:, group]
                     .unsqueeze(3)
-                    .to_broadcast([P, IL, GRAPHS, IL, PAIRS]),
+                    .to_broadcast([P, SENDERS, GRAPHS, IL, PAIRS]),
                 )
                 nc.vector.quantize_mx(
-                    out=sender_codes[:, h, g].rearrange("p l r -> p (l r)").bitcast(FP8X4),
-                    scales=sender_scales[:, h, g].rearrange("p l r -> p (l r)"),
+                    out=sender_codes[:, h, g, group].rearrange("p l r -> p (l r)").bitcast(FP8X4),
+                    scales=sender_scales[:, h, g, group].rearrange("p l r -> p (l r)"),
                     in_=repeated[:],
                 )
 
         def sender(j):
             return sender_codes[:, j // IL, :, j % IL, :], sender_scales[:, j // IL, :, j % IL, :]
 
+        def multiply_nodes(h, name, rows, n):
+            bank = sum_psum.tile([P, BANK], F32, name="product", tag=("soft_bank", "gated_bank")[n])
+            mx_group(bank[:], ((x_codes[:, h], x_scales[:, h], name),), n)
+            nc.scalar.copy(out=rows[:, n * BANK : (n + 1) * BANK], in_=bank[:])
+
+        receiver_rows = [keep.tile([P, C], F32, name="receiver_rows_%d" % h) for h in range(HALVES)]
+        own_rows = [keep.tile([P, C], F32, name="own_rows_%d" % h) for h in range(HALVES)]
+
+        def park_senders():
+            for h in range(HALVES):
+                product = work.tile([P, C], F32, name="product", tag="agg", bufs=AGG_BUFS)
+                for n in range(BANKS):
+                    multiply_nodes(h, "WV", product, n)
+                nc.sync.dma_start(out=x_out_rows[h], in_=product[:])
+
+        sent = {}
+
+        def fetch(j):
+            sent[j] = rows_pool.tile([P, C], F32, name="sender", tag="node_rows", align_bytes=64)
+            nc.sync.dma_start(out=sent[j][:], in_=out_0[:, j, :].unsqueeze(1).to_broadcast([GRAPHS, IL, C]))
+
         grouped = {}
         edge_codes = {}
         edge_scales = {}
         agg = {}
         sums = {}
-        squares = {}
-        norm = {}
-        edge_out = {}
+        moments = {}
+        mean = {}
+        mean_sq = {}
+        rstd = {}
         soft = {}
-        sent = {}
-        soft_sum = keep.tile([P, HALVES, C], F32, name="soft_sum")
-        gated_sum = keep.tile([P, HALVES, C], F32, name="gated_sum")
+        gated = {}
+        soft_banks = []
+        gated_banks = []
 
-        def flip(j):
-            grouped[j] = work.tile([P, HALVES, PASSES, P, PACK], BF16, name="grouped", align_bytes=64)
-            for h in range(HALVES):
-                features_to_partitions(edge_sb[j][:, h, :], grouped[j][:, h])
+        def flip(t):
+            grouped[t] = work.tile([P, PASSES, P, PACK], BF16, name="grouped", align_bytes=64)
+            features_to_partitions(edge_sb[t][:], grouped[t])
 
-        def quantise(j):
-            edge_codes[j] = work.tile([P, HALVES, PASSES, P], U32, name="edge_codes", bufs=3, align_bytes=64)
-            edge_scales[j] = work.tile([P, HALVES, PASSES, P], U8, name="edge_scales", bufs=3, align_bytes=64)
+        def quantise(t):
+            edge_codes[t] = work.tile([P, PASSES, P], U32, name="edge_codes", bufs=3, align_bytes=64)
+            edge_scales[t] = work.tile([P, PASSES, P], U8, name="edge_scales", bufs=3, align_bytes=64)
             nc.vector.quantize_mx(
-                out=edge_codes[j][:].rearrange("p h g r -> p (h g r)").bitcast(FP8X4),
-                scales=edge_scales[j][:].rearrange("p h g r -> p (h g r)"),
-                in_=grouped[j][:].rearrange("p h g r t -> p (h g r t)"),
+                out=edge_codes[t][:].rearrange("p g r -> p (g r)").bitcast(FP8X4),
+                scales=edge_scales[t][:].rearrange("p g r -> p (g r)"),
+                in_=grouped[t][:].rearrange("p g r t -> p (g r t)"),
             )
 
-        def project(j, h):
-            if h == 0:
-                agg[j] = work.tile([P, HALVES, C], F32, name="agg", bufs=3)
-                sums[j] = small.tile([P, HALVES, BANKS], F32, name="sums")
-                squares[j] = small.tile([P, HALVES], F32, name="squares")
-            send_codes, send_scales = sender(j)
-            for n in range(BANKS):
-                cols = slice(n * BANK, (n + 1) * BANK)
-                acc = acc_psum.tile([P, BANK], F32, name="acc")
-                mx_group(
-                    acc[:],
-                    (
-                        (edge_codes[j][:, h], edge_scales[j][:, h], "WE"),
-                        (x_codes[:, h], x_scales[:, h], "WA"),
-                        (send_codes, send_scales, "WB"),
-                    ),
-                    cols,
-                )
-                nc.scalar.activation(
-                    out=agg[j][:, h, cols], in_=acc[:], func=ACT.Identity, accum_out=sums[j][:, h, n : n + 1]
-                )
-            sum_of_squares(agg[j][:, h, :], squares[j][:, h : h + 1])
+        banks_in = {}
 
-        def norm_stats(j):
-            norm[j] = batch_norm(sums[j], squares[j])
-
-        def normalise(j):
-            mean, rstd = norm[j]
-            edge_out[j] = work.tile([P, HALVES, C], F32, name="edge_out")
-            for h in range(HALVES):
-                nc.vector.tensor_scalar(
-                    out=agg[j][:, h, :],
-                    in0=agg[j][:, h, :],
-                    scalar1=mean[:, h : h + 1],
-                    scalar2=0.0,
-                    op0=ALU.subtract,
-                    op1=ALU.max,
-                )
-            for h in range(HALVES):
-                nc.vector.scalar_tensor_tensor(
-                    out=edge_out[j][:, h, :],
-                    in0=agg[j][:, h, :],
-                    scalar=rstd[:, h : h + 1],
-                    in1=edge_sb[j][:, h, :],
-                    op0=ALU.mult,
-                    op1=ALU.add,
-                )
-                nc.sync.dma_start(out=edge_out_rows[h, j], in_=edge_out[j][:, h, :])
-
-        def squash(j):
-            soft[j] = soft_sum if j == 0 else work.tile([P, HALVES, C], F32, name="soft")
-            nc.scalar.activation(out=soft[j][:], in_=edge_out[j][:], func=ACT.Tanh, scale=0.5)
-
-        def exponentiate(j):
-            nc.scalar.activation(out=soft[j][:], in_=soft[j][:], func=ACT.Exp, scale=0.5)
-
-        def add_soft(j):
-            if j > 0:
-                nc.vector.tensor_tensor(out=soft_sum[:], in0=soft_sum[:], in1=soft[j][:], op=ALU.add)
-
-        def send(j):
-            send_codes, send_scales = sender(j)
-            sent[j] = []
-            for n in range(BANKS):
-                bank = send_psum.tile([P, BANK], F32, name="sent")
-                mx_group(bank[:], ((send_codes, send_scales, "WV"),), slice(n * BANK, (n + 1) * BANK))
-                sent[j].append(bank)
-
-        def add_gated(j):
-            gated = gated_sum if j == 0 else work.tile([P, HALVES, C], F32, name="gated", bufs=1)
-            for n in range(BANKS):
-                cols = slice(n * BANK, (n + 1) * BANK)
-                nc.vector.tensor_tensor(
-                    out=gated[:, :, cols],
-                    in0=soft[j][:, :, cols],
-                    in1=sent[j][n][:].unsqueeze(1).to_broadcast([P, HALVES, BANK]),
-                    op=ALU.mult,
-                )
-            if j > 0:
-                for n in range(BANKS):
-                    cols = slice(n * BANK, (n + 1) * BANK)
-                    nc.vector.tensor_tensor(
-                        out=gated_sum[:, :, cols], in0=gated_sum[:, :, cols], in1=gated[:, :, cols], op=ALU.add
-                    )
-
-        def due(j):
-            return 0 <= j < NODES
-
-        repeat_senders(0)
-        for j in range(QUANTISE_AHEAD):
-            flip(j)
-            quantise(j)
-        repeat_senders(1)
-        for r in range(NODES + 2):
-            if due(r - 2):
-                squash(r - 2)
-                exponentiate(r - 2)
-            if due(r):
-                project(r, 0)
-            if due(r - 1):
-                normalise(r - 1)
-            if due(r):
-                project(r, 1)
-            if due(r + QUANTISE_AHEAD):
-                flip(r + QUANTISE_AHEAD)
-            if due(r - 2):
-                send(r - 2)
-                add_soft(r - 2)
-            if due(r):
-                with tc.high_priority():
-                    norm_stats(r)
-            if due(r - 2):
-                add_gated(r - 2)
-            if due(r + QUANTISE_AHEAD):
-                quantise(r + QUANTISE_AHEAD)
-            if due(r + LOAD_AHEAD):
-                load(r + LOAD_AHEAD)
-
-        inverse = work.tile([P, HALVES, C], F32, name="inverse", tag="soft")
-        for h in range(HALVES):
-            nc.scalar.activation(out=inverse[:, h, :], in_=soft_sum[:, h, :], func=ACT.Abs_reciprocal_sqrt)
-            nc.scalar.activation(out=inverse[:, h, :], in_=inverse[:, h, :], func=ACT.Square, scale=0.25)
-        x_new = work.tile([P, HALVES, C], F32, name="x_new", tag="agg", bufs=3)
-        x_sums = small.tile([P, HALVES, BANKS], F32, name="x_sums")
-        x_squares = small.tile([P, HALVES], F32, name="x_squares")
-        for h in range(HALVES):
-            nc.vector.tensor_tensor(
-                out=gated_sum[:, h, :], in0=gated_sum[:, h, :], in1=inverse[:, h, :], op=ALU.mult
+        def multiply(t, n):
+            send_codes, send_scales = sender(t % NODES)
+            acc = acc_psum.tile([P, BANK], F32, name="acc")
+            mx_group(
+                acc[:],
+                ((edge_codes[t], edge_scales[t], "WE"), (send_codes, send_scales, "WB")),
+                n,
             )
-            for n in range(BANKS):
-                cols = slice(n * BANK, (n + 1) * BANK)
-                acc = acc_psum.tile([P, BANK], F32, name="acc")
-                mx_group(acc[:], ((x_codes[:, h], x_scales[:, h], "WU"),), cols)
-                nc.vector.scalar_tensor_tensor(
-                    out=x_new[:, h, cols],
-                    in0=gated_sum[:, h, cols],
-                    scalar=1.0,
-                    in1=acc[:],
-                    op0=ALU.mult,
-                    op1=ALU.add,
-                    accum_out=x_sums[:, h, n : n + 1],
-                )
-            sum_of_squares(x_new[:, h, :], x_squares[:, h : h + 1])
-        mean, rstd = batch_norm(x_sums, x_squares)
-        shift = small.tile([P, HALVES], F32, name="shift")
-        nc.vector.scalar_tensor_tensor(
-            out=shift[:], in0=mean[:], scalar=-1.0, in1=rstd[:], op0=ALU.mult, op1=ALU.mult
-        )
-        x_out = work.tile([P, HALVES, C], F32, name="x_out", tag="edge_out")
-        for h in range(HALVES):
+            banks_in[t, n] = acc
+
+        def empty(t, n):
+            if n == 0:
+                agg[t] = work.tile([P, C], F32, name="agg", bufs=AGG_BUFS)
+                sums[t] = small.tile([P, BANKS, 2], F32, name="sums")
+            cols = slice(n * BANK, (n + 1) * BANK)
             nc.vector.scalar_tensor_tensor(
-                out=x_out[:, h, :],
-                in0=x_new[:, h, :],
-                scalar=rstd[:, h : h + 1],
-                in1=x_sb[:, h, :],
+                out=agg[t][:, cols],
+                in0=receiver_rows[t // NODES][:, cols],
+                scalar=1.0,
+                in1=banks_in[t, n][:],
                 op0=ALU.mult,
                 op1=ALU.add,
+                accum_out=sums[t][:, n, 0:1],
             )
-            nc.scalar.activation(
-                out=x_out[:, h, :], in_=x_out[:, h, :], func=ACT.Relu, bias=shift[:, h : h + 1]
+
+        def square(t, n):
+            sum_of_squares(agg[t][:, n * BANK : (n + 1) * BANK], sums[t][:, n, 1:2])
+
+        def take_moments(t):
+            moments[t], mean[t], mean_sq[t] = moments_of(sums[t])
+
+        def deviate(t):
+            rstd[t] = inverse_deviation(moments[t], mean_sq[t])
+
+        def normalise(t):
+            h, j = divmod(t, NODES)
+            nc.vector.tensor_scalar(
+                out=agg[t][:], in0=agg[t][:], scalar1=mean[t][:], scalar2=0.0, op0=ALU.subtract, op1=ALU.max
             )
-            nc.sync.dma_start(out=x_out_rows[h], in_=x_out[:, h, :])
+            nc.vector.scalar_tensor_tensor(
+                out=agg[t][:], in0=agg[t][:], scalar=rstd[t][:], in1=edge_sb[t][:], op0=ALU.mult, op1=ALU.add
+            )
+            nc.sync.dma_start(out=edge_out_rows[h, j], in_=agg[t][:])
+
+        def squash(t):
+            soft[t] = work.tile([P, C], F32, name="soft", bufs=SOFT_BUFS)
+            nc.scalar.activation(out=soft[t][:], in_=agg[t][:], func=ACT.Tanh, scale=0.5)
+
+        def exponentiate(t):
+            nc.scalar.activation(out=soft[t][:], in_=soft[t][:], func=ACT.Exp, scale=0.5)
+
+        def add_up(values, banks, j):
+            for n in range(BANKS):
+                for k in range(BLOCKS):
+                    first = n * BANK + k * P
+                    nc.tensor.matmul(
+                        out=banks[n][:, k, :],
+                        lhsT=values[:, first : first + P],
+                        rhs=ident[:],
+                        is_transpose=True,
+                        start=(j == 0 and k == 0),
+                        stop=(j == NODES - 1 and k == BLOCKS - 1),
+                    )
+
+        def open_banks(banks, name):
+            banks.clear()
+            for n in range(BANKS):
+                bank = sum_psum.tile([P, BLOCKS, P], F32, name=name)
+                banks.append(bank)
+
+        def add_soft(t):
+            if t % NODES == 0:
+                open_banks(soft_banks, "soft_bank")
+            add_up(soft[t], soft_banks, t % NODES)
+
+        def gate(t):
+            gated[t] = work.tile([P, C], F32, name="gated")
+            nc.vector.tensor_tensor(out=gated[t][:], in0=soft[t][:], in1=sent[t % NODES][:], op=ALU.mult)
+
+        def add_gated(t):
+            if t % NODES == 0:
+                open_banks(gated_banks, "gated_bank")
+            add_up(gated[t], gated_banks, t % NODES)
+
+        soft_sum = {}
+        gated_sum = {}
+
+        def keep_soft(h):
+            soft_sum[h] = keep.tile([P, C], F32, name="soft_sum")
+            for n in range(BANKS):
+                cols = slice(n * BANK, (n + 1) * BANK)
+                nc.scalar.copy(out=soft_sum[h][:, cols], in_=soft_banks[n][:].rearrange("p k r -> p (k r)"))
+
+        def keep_gated(h):
+            gated_sum[h] = keep.tile([P, C], F32, name="gated_sum")
+            for n in range(BANKS):
+                cols = slice(n * BANK, (n + 1) * BANK)
+                nc.vector.tensor_copy(out=gated_sum[h][:, cols], in_=gated_banks[n][:].rearrange("p k r -> p (k r)"))
+
+        def due(t):
+            return 0 <= t < TILES
+
+        with tc.manual_schedule(
+            engines={mybir.EngineType.PE, mybir.EngineType.Activation, mybir.EngineType.DVE}
+        ):
+            for h in range(HALVES):
+                features_to_partitions(x_sb[:, h, :], x_grouped[:, h])
+                flip(h)
+            repeat_senders(0)
+            quantise_nodes()
+            quantise(0)
+            for r in range(TILES + 3):
+                if r == 0:
+                    multiply_nodes(0, "WA", receiver_rows[0], 0)
+                if due(r):
+                    multiply(r, 0)
+                if r == 0:
+                    multiply_nodes(0, "WA", receiver_rows[0], 1)
+                if due(r - 1):
+                    take_moments(r - 1)
+                if due(r):
+                    empty(r, 0)
+                if due(r + 1):
+                    quantise(r + 1)
+                if due(r - 1):
+                    deviate(r - 1)
+                if due(r - 2):
+                    exponentiate(r - 2)
+                if due(r):
+                    square(r, 0)
+                    multiply(r, 1)
+                    empty(r, 1)
+                if due(r + 2):
+                    flip(r + 2)
+                if due(r):
+                    square(r, 1)
+                if due(r - 1):
+                    normalise(r - 1)
+                    squash(r - 1)
+                if due(r - 2):
+                    gate(r - 2)
+                if due(r - 3):
+                    add_soft(r - 3)
+                    add_gated(r - 3)
+                if r - 3 == NODES - 1:
+                    keep_soft(0)
+                    keep_gated(0)
+                if r == 0:
+                    park_senders()
+                    repeat_senders(SENDERS)
+                if r == 1:
+                    for n in range(BANKS):
+                        multiply_nodes(1, "WA", receiver_rows[1], n)
+                    for n in range(BANKS):
+                        multiply_nodes(0, "WU", own_rows[0], n)
+                    repeat_senders(2 * SENDERS)
+                if r == 2:
+                    for n in range(BANKS):
+                        multiply_nodes(1, "WU", own_rows[1], n)
+                    repeat_senders(3 * SENDERS)
+                if r < NODES:
+                    fetch(r)
+                if due(r + LOAD_AHEAD):
+                    load(r + LOAD_AHEAD)
+
+            inverse = {}
+            x_new = {}
+            x_sums = {}
+            for h in range(HALVES):
+                inverse[h] = work.tile([P, C], F32, name="inverse", tag="soft", bufs=SOFT_BUFS)
+                for n in range(BANKS):
+                    cols = slice(n * BANK, (n + 1) * BANK)
+                    softs = soft_sum[0][:, cols] if h == 0 else soft_banks[n][:].rearrange("p k r -> p (k r)")
+                    nc.scalar.activation(out=inverse[h][:, cols], in_=softs, func=ACT.Abs_reciprocal_sqrt)
+                    nc.scalar.activation(
+                        out=inverse[h][:, cols], in_=inverse[h][:, cols], func=ACT.Square, scale=0.25
+                    )
+            for h in range(HALVES):
+                ratio = work.tile([P, C], F32, name="ratio", tag="gated")
+                x_new[h] = work.tile([P, C], F32, name="x_new", tag="agg", bufs=AGG_BUFS)
+                x_sums[h] = small.tile([P, BANKS, 2], F32, name="x_sums", tag="sums")
+                back = []
+                for n in range(BANKS):
+                    cols = slice(n * BANK, (n + 1) * BANK)
+                    gates = gated_sum[0][:, cols] if h == 0 else gated_banks[n][:].rearrange("p k r -> p (k r)")
+                    nc.vector.tensor_tensor(
+                        out=ratio[:, cols], in0=inverse[h][:, cols], in1=gates, op=ALU.mult
+                    )
+                    bank = acc_psum.tile([P, BANK], F32, name="back", tag="acc")
+                    for k in range(BLOCKS):
+                        first = n * BANK + k * P
+                        nc.tensor.transpose(bank[:, k * P : (k + 1) * P], ratio[:, first : first + P], ident[:])
+                    back.append(bank)
+                for n in range(BANKS):
+                    cols = slice(n * BANK, (n + 1) * BANK)
+                    nc.vector.scalar_tensor_tensor(
+                        out=x_new[h][:, cols],
+                        in0=own_rows[h][:, cols],
+                        scalar=1.0,
+                        in1=back[n][:],
+                        op0=ALU.mult,
+                        op1=ALU.add,
+                        accum_out=x_sums[h][:, n, 0:1],
+                    )
+                    sum_of_squares(x_new[h][:, cols], x_sums[h][:, n, 1:2])
+            x_mean = {}
+            x_rstd = {}
+            for h in range(HALVES):
+                x_moments, x_mean[h], x_mean_sq = moments_of(x_sums[h])
+                x_rstd[h] = inverse_deviation(x_moments, x_mean_sq)
+            for h in range(HALVES):
+                shift = small.tile([P, 1], F32, name="shift")
+                nc.vector.scalar_tensor_tensor(
+                    out=shift[:], in0=x_mean[h][:], scalar=-1.0, in1=x_rstd[h][:], op0=ALU.mult, op1=ALU.mult
+                )
+                nc.vector.scalar_tensor_tensor(
+                    out=x_new[h][:],
+                    in0=x_new[h][:],
+                    scalar=x_rstd[h][:],
+                    in1=x_sb[:, h, :],
+                    op0=ALU.mult,
+                    op1=ALU.add,
+                )
+                nc.scalar.activation(out=x_new[h][:], in_=x_new[h][:], func=ACT.Relu, bias=shift[:])
+                nc.sync.dma_start(out=x_out_rows[h], in_=x_new[h][:])

@@ -29,7 +29,9 @@ BLOCKS = BANK // P
 TILES = HALVES * NODES
 LOAD_AHEAD = 4
 SENDERS = 4
-SOFT_BUFS = 3
+SOFT_BUFS = 4
+SUMS = 4
+GATED_BUFS = 3
 AGG_BUFS = 5
 
 LASTING = ("WE", "WB")
@@ -129,9 +131,8 @@ def tile_graphmodel_pa_t_kernel(
             flat = grouped.rearrange("p g r t -> p (g r t)").bitcast(F32)
             return flat.rearrange("p (g r u) -> p g r u", g=PASSES, u=PAIRS)
 
-        def features_to_partitions(rows, grouped):
+        def features_to_partitions(rows, grouped, flipped):
             words = rows.bitcast(F32)
-            flipped = flip_psum.tile([P, PASSES, PAIRS, P], F32, name="flipped")
             for g in range(PASSES):
                 for u in range(PAIRS):
                     nc.tensor.transpose(
@@ -141,34 +142,26 @@ def tile_graphmodel_pa_t_kernel(
                     )
             nc.scalar.copy(out=as_words(grouped), in_=flipped[:].rearrange("p g u r -> p g r u"))
 
+        norm_sums = []
+        for k in range(SUMS):
+            tile = keep.tile([P, BANKS, 2], F32, name="norm_sums_%d" % k)
+            nc.vector.memset(tile[:, 1, 1:2], C * BN_EPS)
+            norm_sums.append(tile)
+
         def moments_of(sums):
-            moments = stat_psum.tile([P, 2], F32, name="moments")
+            bank = stat_psum.tile([P, 2], F32, name="moments")
             for n in range(BANKS):
                 nc.tensor.matmul(
-                    out=moments[:], lhsT=group_mean[:], rhs=sums[:, n, :], start=(n == 0), stop=(n == BANKS - 1)
+                    out=bank[:], lhsT=group_mean[:], rhs=sums[:, n, :], start=(n == 0), stop=(n == BANKS - 1)
                 )
-            mean = small.tile([P, 1], F32, name="mean")
-            nc.scalar.activation(out=mean[:], in_=moments[:, 0:1], func=ACT.Identity)
+            moments = small.tile([P, 2], F32, name="moments_sb")
+            nc.scalar.activation(out=moments[:], in_=bank[:], func=ACT.Identity)
             mean_sq = small.tile([P, 1], F32, name="mean_sq")
-            nc.scalar.activation(out=mean_sq[:], in_=moments[:, 0:1], func=ACT.Square)
-            return moments, mean, mean_sq
-
-        def inverse_deviation(moments, mean_sq):
-            var_eps = small.tile([P, 1], F32, name="var_eps")
-            nc.vector.scalar_tensor_tensor(
-                out=var_eps[:],
-                in0=moments[:, 1:2],
-                scalar=BN_EPS,
-                in1=mean_sq[:],
-                op0=ALU.add,
-                op1=ALU.subtract,
-            )
-            rstd = small.tile([P, 1], F32, name="rstd")
-            nc.gpsimd.tensor_tensor(out=rstd[:], in0=var_eps[:], in1=minus_half[:], op=ALU.pow)
-            return rstd
+            nc.scalar.activation(out=mean_sq[:], in_=bank[:, 0:1], func=ACT.Square)
+            return moments, mean_sq
 
         def sum_of_squares(values, squares_col):
-            unread = work.tile([P, BANK], BF16, name="unread")
+            unread = work.tile([P, C], BF16, name="unread")
             nc.scalar.activation(out=unread[:], in_=values, func=ACT.Square, accum_out=squares_col)
 
         x_sb = keep.tile([P, HALVES, C], BF16, name="x_sb")
@@ -185,17 +178,20 @@ def tile_graphmodel_pa_t_kernel(
         load(0)
         for name in ("WE", "WA", "WB"):
             load_scales(name)
-        load_words("WE", 0)
+        for name in ("WE", "WA", "WB"):
+            load_words(name, 0)
         load(1)
-        for name, n in (("WA", 0), ("WB", 0), ("WE", 1), ("WA", 1), ("WB", 1)):
-            load_words(name, n)
-        for t in range(2, LOAD_AHEAD):
-            load(t)
+        for name in ("WE", "WA", "WB"):
+            load_words(name, 1)
+        load(2)
         for name in ("WV", "WU"):
             load_scales(name)
-        for name in ("WV", "WU"):
-            for n in range(BANKS):
-                load_words(name, n)
+        for n in range(BANKS):
+            load_words("WV", n)
+        load(3)
+        for n in range(BANKS):
+            load_words("WU", n)
+        assert LOAD_AHEAD == 4
 
         ident = keep.tile([P, P], F32, name="ident")
         make_identity(nc, ident[:])
@@ -226,25 +222,29 @@ def tile_graphmodel_pa_t_kernel(
         sender_codes = keep.tile([P, HALVES, PASSES, IL, P], U32, name="sender_codes", align_bytes=64)
         sender_scales = keep.tile([P, HALVES, PASSES, IL, P], U8, name="sender_scales", align_bytes=64)
 
-        def repeat_senders(first):
+        repeated = {}
+
+        def repeat_senders(first, g, copy):
+            h, l = divmod(first, IL)
+            repeated[first, g] = work.tile([P, SENDERS * P * PACK], BF16, name="repeated", align_bytes=64)
+            copy(
+                out=repeated[first, g][:]
+                .bitcast(F32)
+                .rearrange("p (l b i u) -> p l b i u", l=SENDERS, b=GRAPHS, i=IL),
+                in_=as_words(x_grouped[:, h])[:, g]
+                .rearrange("p (b l) u -> p l b u", l=IL)[:, l : l + SENDERS]
+                .unsqueeze(3)
+                .to_broadcast([P, SENDERS, GRAPHS, IL, PAIRS]),
+            )
+
+        def quantise_senders(first, g):
             h, l = divmod(first, IL)
             group = slice(l, l + SENDERS)
-            for g in range(PASSES):
-                repeated = work.tile([P, SENDERS * P * PACK], BF16, name="repeated", align_bytes=64)
-                nc.vector.tensor_copy(
-                    out=repeated[:]
-                    .bitcast(F32)
-                    .rearrange("p (l b i u) -> p l b i u", l=SENDERS, b=GRAPHS, i=IL),
-                    in_=as_words(x_grouped[:, h])[:, g]
-                    .rearrange("p (b l) u -> p l b u", l=IL)[:, group]
-                    .unsqueeze(3)
-                    .to_broadcast([P, SENDERS, GRAPHS, IL, PAIRS]),
-                )
-                nc.vector.quantize_mx(
-                    out=sender_codes[:, h, g, group].rearrange("p l r -> p (l r)").bitcast(FP8X4),
-                    scales=sender_scales[:, h, g, group].rearrange("p l r -> p (l r)"),
-                    in_=repeated[:],
-                )
+            nc.vector.quantize_mx(
+                out=sender_codes[:, h, g, group].rearrange("p l r -> p (l r)").bitcast(FP8X4),
+                scales=sender_scales[:, h, g, group].rearrange("p l r -> p (l r)"),
+                in_=repeated[first, g][:],
+            )
 
         def sender(j):
             return sender_codes[:, j // IL, :, j % IL, :], sender_scales[:, j // IL, :, j % IL, :]
@@ -275,9 +275,7 @@ def tile_graphmodel_pa_t_kernel(
         edge_scales = {}
         agg = {}
         sums = {}
-        moments = {}
         mean = {}
-        mean_sq = {}
         rstd = {}
         soft = {}
         gated = {}
@@ -286,7 +284,8 @@ def tile_graphmodel_pa_t_kernel(
 
         def flip(t):
             grouped[t] = work.tile([P, PASSES, P, PACK], BF16, name="grouped", align_bytes=64)
-            features_to_partitions(edge_sb[t][:], grouped[t])
+            flipped = flip_psum.tile([P, PASSES, PAIRS, P], F32, name="flipped")
+            features_to_partitions(edge_sb[t][:], grouped[t], flipped)
 
         def quantise(t):
             edge_codes[t] = work.tile([P, PASSES, P], U32, name="edge_codes", bufs=3, align_bytes=64)
@@ -312,7 +311,7 @@ def tile_graphmodel_pa_t_kernel(
         def empty(t, n):
             if n == 0:
                 agg[t] = work.tile([P, C], F32, name="agg", bufs=AGG_BUFS)
-                sums[t] = small.tile([P, BANKS, 2], F32, name="sums")
+                sums[t] = norm_sums[t % SUMS]
             cols = slice(n * BANK, (n + 1) * BANK)
             nc.vector.scalar_tensor_tensor(
                 out=agg[t][:, cols],
@@ -324,31 +323,44 @@ def tile_graphmodel_pa_t_kernel(
                 accum_out=sums[t][:, n, 0:1],
             )
 
-        def square(t, n):
-            sum_of_squares(agg[t][:, n * BANK : (n + 1) * BANK], sums[t][:, n, 1:2])
+        def square(t):
+            sum_of_squares(agg[t][:], sums[t][:, 0, 1:2])
 
         def take_moments(t):
-            moments[t], mean[t], mean_sq[t] = moments_of(sums[t])
+            moments, mean_sq = moments_of(sums[t])
+            var_eps = small.tile([P, 1], F32, name="var_eps")
+            nc.scalar.activation(out=var_eps[:], in_=mean_sq[:], func=ACT.Identity, scale=-1.0, bias=moments[:, 1:2])
+            mean[t] = moments[:, 0:1]
+            rstd[t] = small.tile([P, 1], F32, name="rstd")
+            nc.gpsimd.tensor_tensor(out=rstd[t][:], in0=var_eps[:], in1=minus_half[:], op=ALU.pow)
 
-        def deviate(t):
-            rstd[t] = inverse_deviation(moments[t], mean_sq[t])
+        WHOLE = (slice(0, C),)
+        BY_BANK = tuple(slice(n * BANK, (n + 1) * BANK) for n in range(BANKS))
 
-        def normalise(t):
+        def normalise(t, parts):
             h, j = divmod(t, NODES)
             nc.vector.tensor_scalar(
-                out=agg[t][:], in0=agg[t][:], scalar1=mean[t][:], scalar2=0.0, op0=ALU.subtract, op1=ALU.max
+                out=agg[t][:], in0=agg[t][:], scalar1=mean[t], scalar2=0.0, op0=ALU.subtract, op1=ALU.max
             )
-            nc.vector.scalar_tensor_tensor(
-                out=agg[t][:], in0=agg[t][:], scalar=rstd[t][:], in1=edge_sb[t][:], op0=ALU.mult, op1=ALU.add
-            )
+            for cols in parts:
+                nc.vector.scalar_tensor_tensor(
+                    out=agg[t][:, cols],
+                    in0=agg[t][:, cols],
+                    scalar=rstd[t][:],
+                    in1=edge_sb[t][:, cols],
+                    op0=ALU.mult,
+                    op1=ALU.add,
+                )
             nc.sync.dma_start(out=edge_out_rows[h, j], in_=agg[t][:])
 
-        def squash(t):
+        def squash(t, parts):
             soft[t] = work.tile([P, C], F32, name="soft", bufs=SOFT_BUFS)
-            nc.scalar.activation(out=soft[t][:], in_=agg[t][:], func=ACT.Tanh, scale=0.5)
+            for cols in parts:
+                nc.scalar.activation(out=soft[t][:, cols], in_=agg[t][:, cols], func=ACT.Tanh, scale=0.5)
 
-        def exponentiate(t):
-            nc.scalar.activation(out=soft[t][:], in_=soft[t][:], func=ACT.Exp, scale=0.5)
+        def exponentiate(t, parts):
+            for cols in parts:
+                nc.scalar.activation(out=soft[t][:, cols], in_=soft[t][:, cols], func=ACT.Exp, scale=0.5)
 
         def add_up(values, banks, j):
             for n in range(BANKS):
@@ -374,29 +386,107 @@ def tile_graphmodel_pa_t_kernel(
                 open_banks(soft_banks, "soft_bank")
             add_up(soft[t], soft_banks, t % NODES)
 
-        def gate(t):
-            gated[t] = work.tile([P, C], F32, name="gated")
-            nc.vector.tensor_tensor(out=gated[t][:], in0=soft[t][:], in1=sent[t % NODES][:], op=ALU.mult)
+        def gate(t, parts):
+            gated[t] = work.tile([P, C], F32, name="gated", bufs=GATED_BUFS)
+            for cols in parts:
+                nc.vector.tensor_tensor(
+                    out=gated[t][:, cols], in0=soft[t][:, cols], in1=sent[t % NODES][:, cols], op=ALU.mult
+                )
 
         def add_gated(t):
             if t % NODES == 0:
                 open_banks(gated_banks, "gated_bank")
             add_up(gated[t], gated_banks, t % NODES)
 
-        soft_sum = {}
+        soft_squared = {}
         gated_sum = {}
 
         def keep_soft(h):
-            soft_sum[h] = keep.tile([P, C], F32, name="soft_sum")
+            soft_squared[h] = keep.tile([P, C], F32, name="soft_squared_%d" % h)
             for n in range(BANKS):
-                cols = slice(n * BANK, (n + 1) * BANK)
-                nc.scalar.copy(out=soft_sum[h][:, cols], in_=soft_banks[n][:].rearrange("p k r -> p (k r)"))
+                nc.scalar.activation(
+                    out=soft_squared[h][:, n * BANK : (n + 1) * BANK],
+                    in_=soft_banks[n][:].rearrange("p k r -> p (k r)"),
+                    func=ACT.Square,
+                    scale=float(NODES),
+                )
 
         def keep_gated(h):
             gated_sum[h] = keep.tile([P, C], F32, name="gated_sum")
             for n in range(BANKS):
                 cols = slice(n * BANK, (n + 1) * BANK)
                 nc.vector.tensor_copy(out=gated_sum[h][:, cols], in_=gated_banks[n][:].rearrange("p k r -> p (k r)"))
+
+        inverse = {}
+        ratio = {}
+        back = {}
+        x_new = {}
+        x_sums = {}
+        x_mean = {}
+        x_rstd = {}
+
+        def invert(h):
+            inverse[h] = work.tile([P, C], F32, name="inverse", tag="soft", bufs=SOFT_BUFS)
+            for cols in BY_BANK:
+                nc.scalar.activation(
+                    out=inverse[h][:, cols], in_=soft_squared[h][:, cols], func=ACT.Abs_reciprocal_sqrt
+                )
+
+        def divide(h):
+            ratio[h] = work.tile([P, C], F32, name="ratio", tag="gated", bufs=GATED_BUFS)
+            for n, cols in enumerate(BY_BANK):
+                gates = gated_sum[0][:, cols] if h == 0 else gated_banks[n][:].rearrange("p k r -> p (k r)")
+                nc.vector.tensor_tensor(out=ratio[h][:, cols], in0=inverse[h][:, cols], in1=gates, op=ALU.mult)
+                back[h, n] = acc_psum.tile([P, BANK], F32, name="back", tag="acc")
+                for k in range(BLOCKS):
+                    first = n * BANK + k * P
+                    nc.tensor.transpose(
+                        back[h, n][:, k * P : (k + 1) * P], ratio[h][:, first : first + P], ident[:]
+                    )
+
+        def renew(h):
+            x_new[h] = work.tile([P, C], F32, name="x_new", tag="agg", bufs=AGG_BUFS)
+            x_sums[h] = norm_sums[h]
+            for n, cols in enumerate(BY_BANK):
+                nc.vector.scalar_tensor_tensor(
+                    out=x_new[h][:, cols],
+                    in0=own_rows[h][:, cols],
+                    scalar=1.0,
+                    in1=back[h, n][:],
+                    op0=ALU.mult,
+                    op1=ALU.add,
+                    accum_out=x_sums[h][:, n, 0:1],
+                )
+
+        def square_nodes(h):
+            sum_of_squares(x_new[h][:], x_sums[h][:, 0, 1:2])
+
+        def take_node_moments(h):
+            moments, mean_sq = moments_of(x_sums[h])
+            x_mean[h] = moments[:, 0:1]
+            x_rstd[h] = small.tile([P, 1], F32, name="x_rstd")
+            nc.scalar.activation(
+                out=x_rstd[h][:], in_=mean_sq[:], func=ACT.Abs_reciprocal_sqrt, scale=-1.0, bias=moments[:, 1:2]
+            )
+
+        def finish(h):
+            shift = small.tile([P, 1], F32, name="shift")
+            nc.vector.scalar_tensor_tensor(
+                out=shift[:], in0=x_mean[h], scalar=-1.0, in1=x_rstd[h][:], op0=ALU.mult, op1=ALU.mult
+            )
+            for cols in BY_BANK:
+                nc.vector.scalar_tensor_tensor(
+                    out=x_new[h][:, cols],
+                    in0=x_new[h][:, cols],
+                    scalar=x_rstd[h][:],
+                    in1=x_sb[:, h, cols],
+                    op0=ALU.mult,
+                    op1=ALU.add,
+                )
+                nc.scalar.activation(
+                    out=x_new[h][:, cols], in_=x_new[h][:, cols], func=ACT.Relu, bias=shift[:]
+                )
+                nc.sync.dma_start(out=x_out_rows[h][:, :, cols], in_=x_new[h][:, cols])
 
         def due(t):
             return 0 <= t < TILES
@@ -405,122 +495,96 @@ def tile_graphmodel_pa_t_kernel(
             engines={mybir.EngineType.PE, mybir.EngineType.Activation, mybir.EngineType.DVE}
         ):
             for h in range(HALVES):
-                features_to_partitions(x_sb[:, h, :], x_grouped[:, h])
-                flip(h)
-            repeat_senders(0)
+                flipped = sum_psum.tile([P, PASSES, PAIRS, P], F32, name="nodes_flipped", tag="soft_bank")
+                features_to_partitions(x_sb[:, h, :], x_grouped[:, h], flipped)
+            for g in range(PASSES):
+                repeat_senders(0, g, nc.vector.tensor_copy)
+                quantise_senders(0, g)
+            flip(0)
             quantise_nodes()
             quantise(0)
-            for r in range(TILES + 3):
+            for g in range(PASSES):
+                repeat_senders(SENDERS, g, nc.scalar.copy)
+                quantise_senders(SENDERS, g)
+            multiply_nodes(0, "WA", receiver_rows[0], 0)
+            for r in range(TILES):
+                multiply(r, 0)
                 if r == 0:
-                    multiply_nodes(0, "WA", receiver_rows[0], 0)
-                if due(r):
-                    multiply(r, 0)
-                if r == 0:
+                    flip(1)
                     multiply_nodes(0, "WA", receiver_rows[0], 1)
                 if due(r - 1):
                     take_moments(r - 1)
-                if due(r):
-                    empty(r, 0)
+                empty(r, 0)
                 if due(r + 1):
                     quantise(r + 1)
-                if due(r - 1):
-                    deviate(r - 1)
                 if due(r - 2):
-                    exponentiate(r - 2)
-                if due(r):
-                    square(r, 0)
-                    multiply(r, 1)
-                    empty(r, 1)
+                    exponentiate(r - 2, WHOLE)
+                multiply(r, 1)
+                empty(r, 1)
                 if due(r + 2):
                     flip(r + 2)
-                if due(r):
-                    square(r, 1)
+                square(r)
+                if r == 1:
+                    park_senders()
+                if r == 2:
+                    for h in range(HALVES):
+                        for n in range(BANKS):
+                            multiply_nodes(h, "WU", own_rows[h], n)
+                if r == TILES - 1:
+                    take_moments(r)
                 if due(r - 1):
-                    normalise(r - 1)
-                    squash(r - 1)
-                if due(r - 2):
-                    gate(r - 2)
+                    normalise(r - 1, WHOLE)
+                    squash(r - 1, WHOLE)
+                if r == 3:
+                    gate(0, WHOLE)
+                if r > 2:
+                    gate(r - 2, WHOLE)
                 if due(r - 3):
                     add_soft(r - 3)
+                if r == 4:
+                    add_gated(0)
+                if r > 3:
                     add_gated(r - 3)
                 if r - 3 == NODES - 1:
                     keep_soft(0)
                     keep_gated(0)
                 if r == 0:
-                    park_senders()
-                    repeat_senders(SENDERS)
-                if r == 1:
                     for n in range(BANKS):
                         multiply_nodes(1, "WA", receiver_rows[1], n)
-                    for n in range(BANKS):
-                        multiply_nodes(0, "WU", own_rows[0], n)
-                    repeat_senders(2 * SENDERS)
-                if r == 2:
-                    for n in range(BANKS):
-                        multiply_nodes(1, "WU", own_rows[1], n)
-                    repeat_senders(3 * SENDERS)
-                if r < NODES:
-                    fetch(r)
+                if r < HALVES:
+                    for g in range(PASSES):
+                        repeat_senders(IL + r * SENDERS, g, nc.vector.tensor_copy)
+                        quantise_senders(IL + r * SENDERS, g)
+                if r == 1:
+                    fetch(0)
+                    fetch(1)
+                if 1 <= r < NODES - 1:
+                    fetch(r + 1)
                 if due(r + LOAD_AHEAD):
                     load(r + LOAD_AHEAD)
 
-            inverse = {}
-            x_new = {}
-            x_sums = {}
-            for h in range(HALVES):
-                inverse[h] = work.tile([P, C], F32, name="inverse", tag="soft", bufs=SOFT_BUFS)
-                for n in range(BANKS):
-                    cols = slice(n * BANK, (n + 1) * BANK)
-                    softs = soft_sum[0][:, cols] if h == 0 else soft_banks[n][:].rearrange("p k r -> p (k r)")
-                    nc.scalar.activation(out=inverse[h][:, cols], in_=softs, func=ACT.Abs_reciprocal_sqrt)
-                    nc.scalar.activation(
-                        out=inverse[h][:, cols], in_=inverse[h][:, cols], func=ACT.Square, scale=0.25
-                    )
-            for h in range(HALVES):
-                ratio = work.tile([P, C], F32, name="ratio", tag="gated")
-                x_new[h] = work.tile([P, C], F32, name="x_new", tag="agg", bufs=AGG_BUFS)
-                x_sums[h] = small.tile([P, BANKS, 2], F32, name="x_sums", tag="sums")
-                back = []
-                for n in range(BANKS):
-                    cols = slice(n * BANK, (n + 1) * BANK)
-                    gates = gated_sum[0][:, cols] if h == 0 else gated_banks[n][:].rearrange("p k r -> p (k r)")
-                    nc.vector.tensor_tensor(
-                        out=ratio[:, cols], in0=inverse[h][:, cols], in1=gates, op=ALU.mult
-                    )
-                    bank = acc_psum.tile([P, BANK], F32, name="back", tag="acc")
-                    for k in range(BLOCKS):
-                        first = n * BANK + k * P
-                        nc.tensor.transpose(bank[:, k * P : (k + 1) * P], ratio[:, first : first + P], ident[:])
-                    back.append(bank)
-                for n in range(BANKS):
-                    cols = slice(n * BANK, (n + 1) * BANK)
-                    nc.vector.scalar_tensor_tensor(
-                        out=x_new[h][:, cols],
-                        in0=own_rows[h][:, cols],
-                        scalar=1.0,
-                        in1=back[n][:],
-                        op0=ALU.mult,
-                        op1=ALU.add,
-                        accum_out=x_sums[h][:, n, 0:1],
-                    )
-                    sum_of_squares(x_new[h][:, cols], x_sums[h][:, n, 1:2])
-            x_mean = {}
-            x_rstd = {}
-            for h in range(HALVES):
-                x_moments, x_mean[h], x_mean_sq = moments_of(x_sums[h])
-                x_rstd[h] = inverse_deviation(x_moments, x_mean_sq)
-            for h in range(HALVES):
-                shift = small.tile([P, 1], F32, name="shift")
-                nc.vector.scalar_tensor_tensor(
-                    out=shift[:], in0=x_mean[h][:], scalar=-1.0, in1=x_rstd[h][:], op0=ALU.mult, op1=ALU.mult
-                )
-                nc.vector.scalar_tensor_tensor(
-                    out=x_new[h][:],
-                    in0=x_new[h][:],
-                    scalar=x_rstd[h][:],
-                    in1=x_sb[:, h, :],
-                    op0=ALU.mult,
-                    op1=ALU.add,
-                )
-                nc.scalar.activation(out=x_new[h][:], in_=x_new[h][:], func=ACT.Relu, bias=shift[:])
-                nc.sync.dma_start(out=x_out_rows[h], in_=x_new[h][:])
+            last = TILES - 1
+            exponentiate(last - 1, WHOLE)
+            normalise(last, BY_BANK)
+            squash(last, BY_BANK)
+            gate(last - 1, WHOLE)
+            add_soft(last - 2)
+            add_gated(last - 2)
+            exponentiate(last, BY_BANK)
+            gate(last, BY_BANK)
+            for t in (last - 1, last):
+                add_soft(t)
+                add_gated(t)
+            invert(0)
+            keep_soft(1)
+            invert(1)
+            divide(0)
+            renew(0)
+            divide(1)
+            renew(1)
+            square_nodes(0)
+            take_node_moments(0)
+            square_nodes(1)
+            finish(0)
+            take_node_moments(1)
+            finish(1)

@@ -337,11 +337,13 @@ def tile_graphmodel_pa_t_kernel(
         WHOLE = (slice(0, C),)
         BY_BANK = tuple(slice(n * BANK, (n + 1) * BANK) for n in range(BANKS))
 
-        def normalise(t, parts):
-            h, j = divmod(t, NODES)
+        def rectify(t):
             nc.vector.tensor_scalar(
                 out=agg[t][:], in0=agg[t][:], scalar1=mean[t], scalar2=0.0, op0=ALU.subtract, op1=ALU.max
             )
+
+        def add_residual(t, parts):
+            h, j = divmod(t, NODES)
             for cols in parts:
                 nc.vector.scalar_tensor_tensor(
                     out=agg[t][:, cols],
@@ -520,6 +522,8 @@ def tile_graphmodel_pa_t_kernel(
                 if due(r - 2):
                     exponentiate(r - 2, WHOLE)
                 multiply(r, 1)
+                if due(r - 1):
+                    rectify(r - 1)
                 empty(r, 1)
                 if due(r + 2):
                     flip(r + 2)
@@ -533,7 +537,7 @@ def tile_graphmodel_pa_t_kernel(
                 if r == TILES - 1:
                     take_moments(r)
                 if due(r - 1):
-                    normalise(r - 1, WHOLE)
+                    add_residual(r - 1, WHOLE)
                     squash(r - 1, WHOLE)
                 if r == 3:
                     gate(0, WHOLE)
@@ -565,7 +569,8 @@ def tile_graphmodel_pa_t_kernel(
 
             last = TILES - 1
             exponentiate(last - 1, WHOLE)
-            normalise(last, BY_BANK)
+            rectify(last)
+            add_residual(last, BY_BANK)
             squash(last, BY_BANK)
             gate(last - 1, WHOLE)
             add_soft(last - 2)

@@ -29,8 +29,8 @@ BLOCKS = BANK // P
 TILES = HALVES * NODES
 LOAD_AHEAD = 4
 SENDERS = 4
-SOFT_BUFS = 4
-SUMS = 4
+WARM_UP = 32
+SOFT_BUFS = 5
 GATED_BUFS = 3
 AGG_BUFS = 5
 
@@ -142,23 +142,27 @@ def tile_graphmodel_pa_t_kernel(
                     )
             nc.scalar.copy(out=as_words(grouped), in_=flipped[:].rearrange("p g u r -> p g r u"))
 
-        norm_sums = []
-        for k in range(SUMS):
-            tile = keep.tile([P, BANKS, 2], F32, name="norm_sums_%d" % k)
-            nc.vector.memset(tile[:, 1, 1:2], C * BN_EPS)
-            norm_sums.append(tile)
-
         def moments_of(sums):
-            bank = stat_psum.tile([P, 2], F32, name="moments")
-            for n in range(BANKS):
-                nc.tensor.matmul(
-                    out=bank[:], lhsT=group_mean[:], rhs=sums[:, n, :], start=(n == 0), stop=(n == BANKS - 1)
-                )
-            moments = small.tile([P, 2], F32, name="moments_sb")
-            nc.scalar.activation(out=moments[:], in_=bank[:], func=ACT.Identity)
+            bank = stat_psum.tile([P, BANKS + 1], F32, name="bank", tag="moments")
+            nc.tensor.matmul(out=bank[:], lhsT=group_mean[:], rhs=sums[:], start=True, stop=True)
+            parts = small.tile([P, BANKS], F32, name="parts")
+            mean = small.tile([P, 1], F32, name="mean")
+            nc.scalar.activation(out=parts[:], in_=bank[:, 0:BANKS], func=ACT.Identity, accum_out=mean[:])
             mean_sq = small.tile([P, 1], F32, name="mean_sq")
-            nc.scalar.activation(out=mean_sq[:], in_=bank[:, 0:1], func=ACT.Square)
-            return moments, mean_sq
+            nc.scalar.activation(out=mean_sq[:], in_=mean[:], func=ACT.Square)
+            return bank, mean, mean_sq
+
+        def variance_of(bank, mean_sq):
+            var_eps = small.tile([P, 1], F32, name="var_eps")
+            nc.vector.scalar_tensor_tensor(
+                out=var_eps[:],
+                in0=bank[:, BANKS:],
+                scalar=BN_EPS,
+                in1=mean_sq[:],
+                op0=ALU.add,
+                op1=ALU.subtract,
+            )
+            return var_eps
 
         def sum_of_squares(values, squares_col):
             unread = work.tile([P, C], BF16, name="unread")
@@ -249,10 +253,10 @@ def tile_graphmodel_pa_t_kernel(
         def sender(j):
             return sender_codes[:, j // IL, :, j % IL, :], sender_scales[:, j // IL, :, j % IL, :]
 
-        def multiply_nodes(h, name, rows, n):
+        def multiply_nodes(h, name, rows, n, copy):
             bank = sum_psum.tile([P, BANK], F32, name="product", tag=("soft_bank", "gated_bank")[n])
             mx_group(bank[:], ((x_codes[:, h], x_scales[:, h], name),), n)
-            nc.scalar.copy(out=rows[:, n * BANK : (n + 1) * BANK], in_=bank[:])
+            copy(out=rows[:, n * BANK : (n + 1) * BANK], in_=bank[:])
 
         receiver_rows = [keep.tile([P, C], F32, name="receiver_rows_%d" % h) for h in range(HALVES)]
         own_rows = [keep.tile([P, C], F32, name="own_rows_%d" % h) for h in range(HALVES)]
@@ -261,7 +265,7 @@ def tile_graphmodel_pa_t_kernel(
             for h in range(HALVES):
                 product = work.tile([P, C], F32, name="product", tag="agg", bufs=AGG_BUFS)
                 for n in range(BANKS):
-                    multiply_nodes(h, "WV", product, n)
+                    multiply_nodes(h, "WV", product, n, nc.scalar.copy)
                 nc.sync.dma_start(out=x_out_rows[h], in_=product[:])
 
         sent = {}
@@ -275,7 +279,9 @@ def tile_graphmodel_pa_t_kernel(
         edge_scales = {}
         agg = {}
         sums = {}
+        moments = {}
         mean = {}
+        mean_sq = {}
         rstd = {}
         soft = {}
         gated = {}
@@ -311,7 +317,7 @@ def tile_graphmodel_pa_t_kernel(
         def empty(t, n):
             if n == 0:
                 agg[t] = work.tile([P, C], F32, name="agg", bufs=AGG_BUFS)
-                sums[t] = norm_sums[t % SUMS]
+                sums[t] = small.tile([P, BANKS + 1], F32, name="sums")
             cols = slice(n * BANK, (n + 1) * BANK)
             nc.vector.scalar_tensor_tensor(
                 out=agg[t][:, cols],
@@ -320,17 +326,17 @@ def tile_graphmodel_pa_t_kernel(
                 in1=banks_in[t, n][:],
                 op0=ALU.mult,
                 op1=ALU.add,
-                accum_out=sums[t][:, n, 0:1],
+                accum_out=sums[t][:, n : n + 1],
             )
 
         def square(t):
-            sum_of_squares(agg[t][:], sums[t][:, 0, 1:2])
+            sum_of_squares(agg[t][:], sums[t][:, BANKS:])
 
         def take_moments(t):
-            moments, mean_sq = moments_of(sums[t])
-            var_eps = small.tile([P, 1], F32, name="var_eps")
-            nc.scalar.activation(out=var_eps[:], in_=mean_sq[:], func=ACT.Identity, scale=-1.0, bias=moments[:, 1:2])
-            mean[t] = moments[:, 0:1]
+            moments[t], mean[t], mean_sq[t] = moments_of(sums[t])
+
+        def deviate(t):
+            var_eps = variance_of(moments[t], mean_sq[t])
             rstd[t] = small.tile([P, 1], F32, name="rstd")
             nc.gpsimd.tensor_tensor(out=rstd[t][:], in0=var_eps[:], in1=minus_half[:], op=ALU.pow)
 
@@ -339,7 +345,7 @@ def tile_graphmodel_pa_t_kernel(
 
         def rectify(t):
             nc.vector.tensor_scalar(
-                out=agg[t][:], in0=agg[t][:], scalar1=mean[t], scalar2=0.0, op0=ALU.subtract, op1=ALU.max
+                out=agg[t][:], in0=agg[t][:], scalar1=mean[t][:], scalar2=0.0, op0=ALU.subtract, op1=ALU.max
             )
 
         def add_residual(t, parts):
@@ -448,7 +454,7 @@ def tile_graphmodel_pa_t_kernel(
 
         def renew(h):
             x_new[h] = work.tile([P, C], F32, name="x_new", tag="agg", bufs=AGG_BUFS)
-            x_sums[h] = norm_sums[h]
+            x_sums[h] = small.tile([P, BANKS + 1], F32, name="x_sums", tag="sums")
             for n, cols in enumerate(BY_BANK):
                 nc.vector.scalar_tensor_tensor(
                     out=x_new[h][:, cols],
@@ -457,24 +463,22 @@ def tile_graphmodel_pa_t_kernel(
                     in1=back[h, n][:],
                     op0=ALU.mult,
                     op1=ALU.add,
-                    accum_out=x_sums[h][:, n, 0:1],
+                    accum_out=x_sums[h][:, n : n + 1],
                 )
 
         def square_nodes(h):
-            sum_of_squares(x_new[h][:], x_sums[h][:, 0, 1:2])
+            sum_of_squares(x_new[h][:], x_sums[h][:, BANKS:])
 
         def take_node_moments(h):
-            moments, mean_sq = moments_of(x_sums[h])
-            x_mean[h] = moments[:, 0:1]
+            bank, x_mean[h], mean_sq = moments_of(x_sums[h])
+            var_eps = variance_of(bank, mean_sq)
             x_rstd[h] = small.tile([P, 1], F32, name="x_rstd")
-            nc.scalar.activation(
-                out=x_rstd[h][:], in_=mean_sq[:], func=ACT.Abs_reciprocal_sqrt, scale=-1.0, bias=moments[:, 1:2]
-            )
+            nc.scalar.activation(out=x_rstd[h][:], in_=var_eps[:], func=ACT.Abs_reciprocal_sqrt)
 
         def finish(h):
             shift = small.tile([P, 1], F32, name="shift")
             nc.vector.scalar_tensor_tensor(
-                out=shift[:], in0=x_mean[h], scalar=-1.0, in1=x_rstd[h][:], op0=ALU.mult, op1=ALU.mult
+                out=shift[:], in0=x_mean[h][:], scalar=-1.0, in1=x_rstd[h][:], op0=ALU.mult, op1=ALU.mult
             )
             for cols in BY_BANK:
                 nc.vector.scalar_tensor_tensor(
@@ -503,22 +507,27 @@ def tile_graphmodel_pa_t_kernel(
                 repeat_senders(0, g, nc.vector.tensor_copy)
                 quantise_senders(0, g)
             flip(0)
+            warm = stat_psum.tile([P, P], F32, name="warm", tag="moments")
+            for k in range(WARM_UP):
+                nc.tensor.transpose(warm[:], ident[:], ident[:])
             quantise_nodes()
             quantise(0)
             for g in range(PASSES):
                 repeat_senders(SENDERS, g, nc.scalar.copy)
                 quantise_senders(SENDERS, g)
-            multiply_nodes(0, "WA", receiver_rows[0], 0)
+            multiply_nodes(0, "WA", receiver_rows[0], 0, nc.scalar.copy)
             for r in range(TILES):
                 multiply(r, 0)
                 if r == 0:
                     flip(1)
-                    multiply_nodes(0, "WA", receiver_rows[0], 1)
+                    multiply_nodes(0, "WA", receiver_rows[0], 1, nc.scalar.copy)
                 if due(r - 1):
                     take_moments(r - 1)
                 empty(r, 0)
                 if due(r + 1):
                     quantise(r + 1)
+                if due(r - 1):
+                    deviate(r - 1)
                 if due(r - 2):
                     exponentiate(r - 2, WHOLE)
                 multiply(r, 1)
@@ -530,31 +539,26 @@ def tile_graphmodel_pa_t_kernel(
                 square(r)
                 if r == 1:
                     park_senders()
-                if r == 2:
-                    for h in range(HALVES):
-                        for n in range(BANKS):
-                            multiply_nodes(h, "WU", own_rows[h], n)
                 if r == TILES - 1:
                     take_moments(r)
                 if due(r - 1):
                     add_residual(r - 1, WHOLE)
                     squash(r - 1, WHOLE)
-                if r == 3:
-                    gate(0, WHOLE)
-                if r > 2:
-                    gate(r - 2, WHOLE)
+                if r == 2:
+                    for h in range(HALVES):
+                        for n in range(BANKS):
+                            multiply_nodes(h, "WU", own_rows[h], n, nc.vector.tensor_copy)
                 if due(r - 3):
-                    add_soft(r - 3)
-                if r == 4:
-                    add_gated(0)
-                if r > 3:
-                    add_gated(r - 3)
-                if r - 3 == NODES - 1:
+                    gate(r - 3, WHOLE)
+                if due(r - 4):
+                    add_soft(r - 4)
+                    add_gated(r - 4)
+                if r - 4 == NODES - 1:
                     keep_soft(0)
                     keep_gated(0)
                 if r == 0:
                     for n in range(BANKS):
-                        multiply_nodes(1, "WA", receiver_rows[1], n)
+                        multiply_nodes(1, "WA", receiver_rows[1], n, nc.scalar.copy)
                 if r < HALVES:
                     for g in range(PASSES):
                         repeat_senders(IL + r * SENDERS, g, nc.vector.tensor_copy)
@@ -569,12 +573,15 @@ def tile_graphmodel_pa_t_kernel(
 
             last = TILES - 1
             exponentiate(last - 1, WHOLE)
+            deviate(last)
             rectify(last)
             add_residual(last, BY_BANK)
             squash(last, BY_BANK)
+            gate(last - 2, WHOLE)
             gate(last - 1, WHOLE)
-            add_soft(last - 2)
-            add_gated(last - 2)
+            for t in (last - 3, last - 2):
+                add_soft(t)
+                add_gated(t)
             exponentiate(last, BY_BANK)
             gate(last, BY_BANK)
             for t in (last - 1, last):

@@ -32,7 +32,7 @@ SENDERS = 4
 WARM_UP = 32
 SOFT_BUFS = 5
 GATED_BUFS = 3
-AGG_BUFS = 5
+AGG_BUFS = 6
 
 LASTING = ("WE", "WB")
 
@@ -165,7 +165,7 @@ def tile_graphmodel_pa_t_kernel(
             return var_eps
 
         def sum_of_squares(values, squares_col):
-            unread = work.tile([P, C], BF16, name="unread")
+            unread = work.tile([P, C], BF16, name="unread", bufs=1)
             nc.scalar.activation(out=unread[:], in_=values, func=ACT.Square, accum_out=squares_col)
 
         x_sb = keep.tile([P, HALVES, C], BF16, name="x_sb")
@@ -521,44 +521,41 @@ def tile_graphmodel_pa_t_kernel(
                 if r == 0:
                     flip(1)
                     multiply_nodes(0, "WA", receiver_rows[0], 1, nc.scalar.copy)
-                if due(r - 1):
-                    take_moments(r - 1)
                 empty(r, 0)
                 if due(r + 1):
                     quantise(r + 1)
-                if due(r - 1):
-                    deviate(r - 1)
-                if due(r - 2):
-                    exponentiate(r - 2, WHOLE)
                 multiply(r, 1)
-                if due(r - 1):
-                    rectify(r - 1)
                 empty(r, 1)
+                if due(r - 1):
+                    take_moments(r - 1)
+                    deviate(r - 1)
+                    rectify(r - 1)
+                if due(r - 2):
+                    squash(r - 2, WHOLE)
+                square(r)
                 if due(r + 2):
                     flip(r + 2)
-                square(r)
+                if r == 0:
+                    for n in range(BANKS):
+                        multiply_nodes(1, "WA", receiver_rows[1], n, nc.scalar.copy)
                 if r == 1:
                     park_senders()
-                if r == TILES - 1:
-                    take_moments(r)
-                if due(r - 1):
-                    add_residual(r - 1, WHOLE)
-                    squash(r - 1, WHOLE)
                 if r == 2:
                     for h in range(HALVES):
                         for n in range(BANKS):
                             multiply_nodes(h, "WU", own_rows[h], n, nc.vector.tensor_copy)
+                if due(r - 2):
+                    exponentiate(r - 2, WHOLE)
                 if due(r - 3):
                     gate(r - 3, WHOLE)
+                if due(r - 1):
+                    add_residual(r - 1, WHOLE)
                 if due(r - 4):
                     add_soft(r - 4)
                     add_gated(r - 4)
                 if r - 4 == NODES - 1:
                     keep_soft(0)
                     keep_gated(0)
-                if r == 0:
-                    for n in range(BANKS):
-                        multiply_nodes(1, "WA", receiver_rows[1], n, nc.scalar.copy)
                 if r < HALVES:
                     for g in range(PASSES):
                         repeat_senders(IL + r * SENDERS, g, nc.vector.tensor_copy)
@@ -572,17 +569,19 @@ def tile_graphmodel_pa_t_kernel(
                     load(r + LOAD_AHEAD)
 
             last = TILES - 1
-            exponentiate(last - 1, WHOLE)
+            take_moments(last)
             deviate(last)
             rectify(last)
-            add_residual(last, BY_BANK)
-            squash(last, BY_BANK)
+            squash(last - 1, WHOLE)
             gate(last - 2, WHOLE)
-            gate(last - 1, WHOLE)
+            add_residual(last, BY_BANK)
+            exponentiate(last - 1, WHOLE)
+            squash(last, BY_BANK)
+            exponentiate(last, BY_BANK)
             for t in (last - 3, last - 2):
                 add_soft(t)
                 add_gated(t)
-            exponentiate(last, BY_BANK)
+            gate(last - 1, WHOLE)
             gate(last, BY_BANK)
             for t in (last - 1, last):
                 add_soft(t)

@@ -30,7 +30,7 @@ TILES = HALVES * NODES
 LOAD_AHEAD = 4
 SENDERS = 4
 WARM_UP = 32
-SOFT_BUFS = 5
+SOFT_BUFS = 4
 GATED_BUFS = 3
 AGG_BUFS = 6
 
@@ -176,7 +176,7 @@ def tile_graphmodel_pa_t_kernel(
 
         def load(t):
             h, j = divmod(t, NODES)
-            edge_sb[t] = work.tile([P, C], BF16, name="edge_sb", bufs=LOAD_AHEAD + 2)
+            edge_sb[t] = work.tile([P, C], BF16, name="edge_sb", bufs=LOAD_AHEAD + 3)
             nc.sync.dma_start(out=edge_sb[t][:], in_=edge_rows[h, j])
 
         load(0)
@@ -524,17 +524,19 @@ def tile_graphmodel_pa_t_kernel(
                 empty(r, 0)
                 if due(r + 1):
                     quantise(r + 1)
+                if due(r - 2):
+                    add_residual(r - 2, WHOLE)
                 multiply(r, 1)
                 empty(r, 1)
                 if due(r - 1):
                     take_moments(r - 1)
                     deviate(r - 1)
                     rectify(r - 1)
-                if due(r - 2):
-                    squash(r - 2, WHOLE)
-                square(r)
+                if due(r - 3):
+                    exponentiate(r - 3, WHOLE)
                 if due(r + 2):
                     flip(r + 2)
+                square(r)
                 if r == 0:
                     for n in range(BANKS):
                         multiply_nodes(1, "WA", receiver_rows[1], n, nc.scalar.copy)
@@ -545,11 +547,9 @@ def tile_graphmodel_pa_t_kernel(
                         for n in range(BANKS):
                             multiply_nodes(h, "WU", own_rows[h], n, nc.vector.tensor_copy)
                 if due(r - 2):
-                    exponentiate(r - 2, WHOLE)
+                    squash(r - 2, WHOLE)
                 if due(r - 3):
                     gate(r - 3, WHOLE)
-                if due(r - 1):
-                    add_residual(r - 1, WHOLE)
                 if due(r - 4):
                     add_soft(r - 4)
                     add_gated(r - 4)
@@ -569,9 +569,11 @@ def tile_graphmodel_pa_t_kernel(
                     load(r + LOAD_AHEAD)
 
             last = TILES - 1
+            add_residual(last - 1, WHOLE)
             take_moments(last)
             deviate(last)
             rectify(last)
+            exponentiate(last - 2, WHOLE)
             squash(last - 1, WHOLE)
             gate(last - 2, WHOLE)
             add_residual(last, BY_BANK)

@@ -524,13 +524,15 @@ def tile_graphmodel_pa_t_kernel(
                 empty(r, 0)
                 if due(r + 1):
                     quantise(r + 1)
+                if due(r - 1):
+                    take_moments(r - 1)
                 if due(r - 2):
                     add_residual(r - 2, WHOLE)
+                if due(r - 1):
+                    deviate(r - 1)
                 multiply(r, 1)
                 empty(r, 1)
                 if due(r - 1):
-                    take_moments(r - 1)
-                    deviate(r - 1)
                     rectify(r - 1)
                 if due(r - 3):
                     exponentiate(r - 3, WHOLE)

@@ -30,7 +30,7 @@ TILES = HALVES * NODES
 LOAD_AHEAD = 4
 SENDERS = 4
 WARM_UP = 32
-SOFT_BUFS = 4
+SOFT_BUFS = 5
 GATED_BUFS = 3
 AGG_BUFS = 6
 
@@ -142,21 +142,25 @@ def tile_graphmodel_pa_t_kernel(
                     )
             nc.scalar.copy(out=as_words(grouped), in_=flipped[:].rearrange("p g u r -> p g r u"))
 
+        def add_parts(parts, name):
+            copied = small.tile([P, BANKS], F32, name="copied_" + name)
+            total = small.tile([P, 1], F32, name=name)
+            nc.scalar.activation(out=copied[:], in_=parts, func=ACT.Identity, accum_out=total[:])
+            return total
+
         def moments_of(sums):
             bank = stat_psum.tile([P, BANKS + 1], F32, name="bank", tag="moments")
             nc.tensor.matmul(out=bank[:], lhsT=group_mean[:], rhs=sums[:], start=True, stop=True)
-            parts = small.tile([P, BANKS], F32, name="parts")
-            mean = small.tile([P, 1], F32, name="mean")
-            nc.scalar.activation(out=parts[:], in_=bank[:, 0:BANKS], func=ACT.Identity, accum_out=mean[:])
+            mean = add_parts(bank[:, 0:BANKS], "mean")
             mean_sq = small.tile([P, 1], F32, name="mean_sq")
             nc.scalar.activation(out=mean_sq[:], in_=mean[:], func=ACT.Square)
             return bank, mean, mean_sq
 
-        def variance_of(bank, mean_sq):
+        def variance_of(square_mean, mean_sq):
             var_eps = small.tile([P, 1], F32, name="var_eps")
             nc.vector.scalar_tensor_tensor(
                 out=var_eps[:],
-                in0=bank[:, BANKS:],
+                in0=square_mean,
                 scalar=BN_EPS,
                 in1=mean_sq[:],
                 op0=ALU.add,
@@ -166,7 +170,9 @@ def tile_graphmodel_pa_t_kernel(
 
         def sum_of_squares(values, squares_col):
             unread = work.tile([P, C], BF16, name="unread", bufs=1)
-            nc.scalar.activation(out=unread[:], in_=values, func=ACT.Square, accum_out=squares_col)
+            nc.scalar.activation(
+                out=unread[:, 0 : values.shape[-1]], in_=values, func=ACT.Square, accum_out=squares_col
+            )
 
         x_sb = keep.tile([P, HALVES, C], BF16, name="x_sb")
         for h in range(HALVES):
@@ -336,7 +342,7 @@ def tile_graphmodel_pa_t_kernel(
             moments[t], mean[t], mean_sq[t] = moments_of(sums[t])
 
         def deviate(t):
-            var_eps = variance_of(moments[t], mean_sq[t])
+            var_eps = variance_of(moments[t][:, BANKS:], mean_sq[t])
             rstd[t] = small.tile([P, 1], F32, name="rstd")
             nc.gpsimd.tensor_tensor(out=rstd[t][:], in0=var_eps[:], in1=minus_half[:], op=ALU.pow)
 
@@ -454,7 +460,7 @@ def tile_graphmodel_pa_t_kernel(
 
         def renew(h):
             x_new[h] = work.tile([P, C], F32, name="x_new", tag="agg", bufs=AGG_BUFS)
-            x_sums[h] = small.tile([P, BANKS + 1], F32, name="x_sums", tag="sums")
+            x_sums[h] = small.tile([P, 2 * BANKS], F32, name="x_sums")
             for n, cols in enumerate(BY_BANK):
                 nc.vector.scalar_tensor_tensor(
                     out=x_new[h][:, cols],
@@ -467,11 +473,17 @@ def tile_graphmodel_pa_t_kernel(
                 )
 
         def square_nodes(h):
-            sum_of_squares(x_new[h][:], x_sums[h][:, BANKS:])
+            for n, cols in enumerate(BY_BANK):
+                sum_of_squares(x_new[h][:, cols], x_sums[h][:, BANKS + n : BANKS + n + 1])
 
         def take_node_moments(h):
-            bank, x_mean[h], mean_sq = moments_of(x_sums[h])
-            var_eps = variance_of(bank, mean_sq)
+            bank = stat_psum.tile([P, 2 * BANKS], F32, name="node_bank", tag="moments")
+            nc.tensor.matmul(out=bank[:], lhsT=group_mean[:], rhs=x_sums[h][:], start=True, stop=True)
+            x_mean[h] = add_parts(bank[:, 0:BANKS], "x_mean")
+            square_mean = add_parts(bank[:, BANKS:], "x_square_mean")
+            mean_sq = small.tile([P, 1], F32, name="x_mean_sq")
+            nc.scalar.activation(out=mean_sq[:], in_=x_mean[h][:], func=ACT.Square)
+            var_eps = variance_of(square_mean[:], mean_sq)
             x_rstd[h] = small.tile([P, 1], F32, name="x_rstd")
             nc.scalar.activation(out=x_rstd[h][:], in_=var_eps[:], func=ACT.Abs_reciprocal_sqrt)
 
@@ -516,6 +528,7 @@ def tile_graphmodel_pa_t_kernel(
                 repeat_senders(SENDERS, g, nc.scalar.copy)
                 quantise_senders(SENDERS, g)
             multiply_nodes(0, "WA", receiver_rows[0], 0, nc.scalar.copy)
+            last = TILES - 1
             for r in range(TILES):
                 multiply(r, 0)
                 if r == 0:
@@ -524,38 +537,39 @@ def tile_graphmodel_pa_t_kernel(
                 empty(r, 0)
                 if due(r + 1):
                     quantise(r + 1)
-                if due(r - 1):
-                    take_moments(r - 1)
-                if due(r - 2):
-                    add_residual(r - 2, WHOLE)
-                if due(r - 1):
-                    deviate(r - 1)
                 multiply(r, 1)
                 empty(r, 1)
                 if due(r - 1):
+                    take_moments(r - 1)
+                if r == last:
                     rectify(r - 1)
-                if due(r - 3):
-                    exponentiate(r - 3, WHOLE)
+                    deviate(r - 1)
+                square(r)
                 if due(r + 2):
                     flip(r + 2)
-                square(r)
                 if r == 0:
                     for n in range(BANKS):
                         multiply_nodes(1, "WA", receiver_rows[1], n, nc.scalar.copy)
                 if r == 1:
                     park_senders()
+                if due(r - 3):
+                    exponentiate(r - 3, WHOLE)
+                if due(r - 4):
+                    gate(r - 4, WHOLE)
+                if due(r - 2):
+                    add_residual(r - 2, WHOLE)
+                    squash(r - 2, WHOLE)
                 if r == 2:
                     for h in range(HALVES):
                         for n in range(BANKS):
                             multiply_nodes(h, "WU", own_rows[h], n, nc.vector.tensor_copy)
-                if due(r - 2):
-                    squash(r - 2, WHOLE)
-                if due(r - 3):
-                    gate(r - 3, WHOLE)
-                if due(r - 4):
-                    add_soft(r - 4)
-                    add_gated(r - 4)
-                if r - 4 == NODES - 1:
+                if due(r - 1) and r < last:
+                    rectify(r - 1)
+                    deviate(r - 1)
+                if due(r - 5):
+                    add_soft(r - 5)
+                    add_gated(r - 5)
+                if r - 5 == NODES - 1:
                     keep_soft(0)
                     keep_gated(0)
                 if r < HALVES:
@@ -570,19 +584,19 @@ def tile_graphmodel_pa_t_kernel(
                 if due(r + LOAD_AHEAD):
                     load(r + LOAD_AHEAD)
 
-            last = TILES - 1
-            add_residual(last - 1, WHOLE)
             take_moments(last)
-            deviate(last)
-            rectify(last)
-            exponentiate(last - 2, WHOLE)
+            add_residual(last - 1, WHOLE)
             squash(last - 1, WHOLE)
-            gate(last - 2, WHOLE)
+            rectify(last)
+            deviate(last)
+            exponentiate(last - 2, WHOLE)
+            gate(last - 3, WHOLE)
             add_residual(last, BY_BANK)
             exponentiate(last - 1, WHOLE)
             squash(last, BY_BANK)
+            gate(last - 2, WHOLE)
             exponentiate(last, BY_BANK)
-            for t in (last - 3, last - 2):
+            for t in (last - 4, last - 3, last - 2):
                 add_soft(t)
                 add_gated(t)
             gate(last - 1, WHOLE)

from contextlib import ExitStack

import concourse.mybir as mybir
from concourse.masks import make_identity

F32 = mybir.dt.float32
BF16 = mybir.dt.bfloat16
I32 = mybir.dt.int32
U32 = mybir.dt.uint32
U8 = mybir.dt.uint8
FP8X4 = mybir.dt.float8_e4m3fn_x4
ACT = mybir.ActivationFunctionType
ALU = mybir.AluOpType
AX = mybir.AxisListType

P = 128
GRAPHS = 16
NODES = 16
C = 1024
HALVES = 2
IL = NODES // HALVES
PACK = 4
PASSES = C // (P * PACK)
PAIRS = PACK // 2
BANK = 512
BANKS = C // BANK
BN_EPS = 1e-5
BLOCKS = BANK // P
TILES = HALVES * NODES
LOAD_AHEAD = 4
SENDERS = 4
WARM_UP = 32
SOFT_BUFS = 5
GATED_BUFS = 3
AGG_BUFS = 6

LASTING = ("WE", "WB")

FLOPS = 2 * (GRAPHS * NODES * NODES + 4 * GRAPHS * NODES) * C * C


def tile_graphmodel_pa_t_kernel(
    tc,
    x,
    edge,
    WA_words,
    WA_scales,
    WB_words,
    WB_scales,
    WE_words,
    WE_scales,
    WU_words,
    WU_scales,
    WV_words,
    WV_scales,
    out_0,
    out_1,
):
    nc = tc.nc

    x_rows = x.rearrange("b (h i) c -> h b i c", h=HALVES)
    x_out_rows = out_0.rearrange("b (h i) c -> h b i c", h=HALVES)
    edge_rows = edge.rearrange("b (h i j) c -> h j b i c", h=HALVES, i=IL)
    edge_out_rows = out_1.rearrange("b (h i j) c -> h j b i c", h=HALVES, i=IL)

    with ExitStack() as ctx:
        keep = ctx.enter_context(tc.tile_pool(name="keep", bufs=1))
        work = ctx.enter_context(tc.tile_pool(name="work", bufs=2))
        small = ctx.enter_context(tc.tile_pool(name="small", bufs=3))
        rows_pool = ctx.enter_context(tc.tile_pool(name="rows_pool", bufs=NODES))
        acc_psum = ctx.enter_context(tc.psum_pool(name="acc_psum", bufs=2))
        flip_psum = ctx.enter_context(tc.psum_pool(name="flip_psum", bufs=1))
        stat_psum = ctx.enter_context(tc.psum_pool(name="stat_psum", bufs=1))
        sum_psum = ctx.enter_context(tc.psum_pool(name="sum_psum", bufs=2))

        given = {
            "WE": (WE_words, WE_scales),
            "WA": (WA_words, WA_scales),
            "WB": (WB_words, WB_scales),
            "WV": (WV_words, WV_scales),
            "WU": (WU_words, WU_scales),
        }
        sharing = (("WE", "WA"), ("WB",), ("WV", "WU"))
        w_words = {}
        w_planes = {}
        for names in sharing:
            planes = keep.tile([P, C], U8, name="planes_" + names[0], align_bytes=64)
            nc.vector.memset(planes[:].bitcast(I32), 0)
            for place, name in enumerate(names):
                w_planes[name] = (planes, PACK * PASSES * place)

        def load_scales(name):
            planes, first = w_planes[name]
            for quad in range(4):
                nc.sync.dma_start(
                    out=planes[32 * quad + first : 32 * quad + first + PACK * PASSES, :].bitcast(I32),
                    in_=given[name][1][:, 4 * quad : 4 * quad + 4, :].bitcast(I32),
                )

        def load_words(name, n):
            if name in LASTING:
                words = keep.tile([P, PASSES, BANK], U32, name="words_%s_%d" % (name, n), align_bytes=64)
            else:
                words = rows_pool.tile([P, PASSES, BANK], U32, name="words", tag="node_rows", align_bytes=64)
            nc.sync.dma_start(
                out=words[:].bitcast(I32),
                in_=given[name][0][:, :, n * BANK : (n + 1) * BANK, :]
                .rearrange("g p n t -> p g (n t)")
                .bitcast(I32),
            )
            w_words[name, n] = words

        def mx_group(acc, terms, n):
            last = len(terms) * PASSES - 1
            done = 0
            for codes, scales, name in terms:
                planes, first = w_planes[name]
                for g in range(PASSES):
                    nc.tensor.matmul_mx(
                        out=acc,
                        lhsT=codes[:, g, :].bitcast(FP8X4),
                        lhsT_scale=scales[:, g, :],
                        rhs=w_words[name, n][:, g, :].bitcast(FP8X4),
                        rhs_scale=planes[first + PACK * g : P, n * BANK : (n + 1) * BANK],
                        start=(done == 0),
                        stop=(done == last),
                    )
                    done += 1

        def as_words(grouped):
            flat = grouped.rearrange("p g r t -> p (g r t)").bitcast(F32)
            return flat.rearrange("p (g r u) -> p g r u", g=PASSES, u=PAIRS)

        def features_to_partitions(rows, grouped, flipped):
            words = rows.bitcast(F32)
            for g in range(PASSES):
                for u in range(PAIRS):
                    nc.tensor.transpose(
                        flipped[:, g, u, :],
                        words[:, (C // 4) * g + u : (C // 4) * (g + 1) : PAIRS],
                        ident[:],
                    )
            nc.scalar.copy(out=as_words(grouped), in_=flipped[:].rearrange("p g u r -> p g r u"))

        def add_parts(parts, name):
            copied = small.tile([P, BANKS], F32, name="copied_" + name)
            total = small.tile([P, 1], F32, name=name)
            nc.scalar.activation(out=copied[:], in_=parts, func=ACT.Identity, accum_out=total[:])
            return total

        def moments_of(sums):
            bank = stat_psum.tile([P, BANKS + 1], F32, name="bank", tag="moments")
            nc.tensor.matmul(out=bank[:], lhsT=group_mean[:], rhs=sums[:], start=True, stop=True)
            mean = add_parts(bank[:, 0:BANKS], "mean")
            mean_sq = small.tile([P, 1], F32, name="mean_sq")
            nc.scalar.activation(out=mean_sq[:], in_=mean[:], func=ACT.Square)
            return bank, mean, mean_sq

        def variance_of(square_mean, mean_sq):
            var_eps = small.tile([P, 1], F32, name="var_eps")
            nc.vector.scalar_tensor_tensor(
                out=var_eps[:],
                in0=square_mean,
                scalar=BN_EPS,
                in1=mean_sq[:],
                op0=ALU.add,
                op1=ALU.subtract,
            )
            return var_eps

        def sum_of_squares(values, squares_col):
            unread = work.tile([P, C], BF16, name="unread", bufs=1)
            nc.scalar.activation(
                out=unread[:, 0 : values.shape[-1]], in_=values, func=ACT.Square, accum_out=squares_col
            )

        x_sb = keep.tile([P, HALVES, C], BF16, name="x_sb")
        for h in range(HALVES):
            nc.sync.dma_start(out=x_sb[:, h, :], in_=x_rows[h])

        edge_sb = {}

        def load(t):
            h, j = divmod(t, NODES)
            edge_sb[t] = work.tile([P, C], BF16, name="edge_sb", bufs=LOAD_AHEAD + 3)
            nc.sync.dma_start(out=edge_sb[t][:], in_=edge_rows[h, j])

        load(0)
        for name in ("WE", "WA", "WB"):
            load_scales(name)
        for name in ("WE", "WA", "WB"):
            load_words(name, 0)
        load(1)
        for name in ("WE", "WA", "WB"):
            load_words(name, 1)
        load(2)
        for name in ("WV", "WU"):
            load_scales(name)
        for n in range(BANKS):
            load_words("WV", n)
        load(3)
        for n in range(BANKS):
            load_words("WU", n)
        assert LOAD_AHEAD == 4

        ident = keep.tile([P, P], F32, name="ident")
        make_identity(nc, ident[:])
        same_il = keep.tile([P, IL], F32, name="same_il")
        nc.vector.tensor_reduce(
            out=same_il[:], in_=ident[:].rearrange("p (b i) -> p i b", i=IL), axis=AX.X, op=ALU.add
        )
        group_mean = keep.tile([P, P], F32, name="group_mean")
        nc.vector.tensor_scalar_mul(
            out=group_mean[:].rearrange("p (b i) -> p b i", i=IL),
            in0=same_il[:].unsqueeze(1).to_broadcast([P, GRAPHS, IL]),
            scalar1=1.0 / (GRAPHS * C),
        )
        minus_half = keep.tile([P, 1], F32, name="minus_half")
        nc.vector.memset(minus_half[:], -0.5)

        x_grouped = keep.tile([P, HALVES, PASSES, P, PACK], BF16, name="x_grouped", align_bytes=64)
        x_codes = keep.tile([P, HALVES, PASSES, P], U32, name="x_codes", align_bytes=64)
        x_scales = keep.tile([P, HALVES, PASSES, P], U8, name="x_scales", align_bytes=64)

        def quantise_nodes():
            nc.vector.quantize_mx(
                out=x_codes[:].rearrange("p h g r -> p (h g r)").bitcast(FP8X4),
                scales=x_scales[:].rearrange("p h g r -> p (h g r)"),
                in_=x_grouped[:].rearrange("p h g r t -> p (h g r t)"),
            )

        sender_codes = keep.tile([P, HALVES, PASSES, IL, P], U32, name="sender_codes", align_bytes=64)
        sender_scales = keep.tile([P, HALVES, PASSES, IL, P], U8, name="sender_scales", align_bytes=64)

        repeated = {}

        def repeat_senders(first, g, copy):
            h, l = divmod(first, IL)
            repeated[first, g] = work.tile([P, SENDERS * P * PACK], BF16, name="repeated", align_bytes=64)
            copy(
                out=repeated[first, g][:]
                .bitcast(F32)
                .rearrange("p (l b i u) -> p l b i u", l=SENDERS, b=GRAPHS, i=IL),
                in_=as_words(x_grouped[:, h])[:, g]
                .rearrange("p (b l) u -> p l b u", l=IL)[:, l : l + SENDERS]
                .unsqueeze(3)
                .to_broadcast([P, SENDERS, GRAPHS, IL, PAIRS]),
            )

        def quantise_senders(first, g):
            h, l = divmod(first, IL)
            group = slice(l, l + SENDERS)
            nc.vector.quantize_mx(
                out=sender_codes[:, h, g, group].rearrange("p l r -> p (l r)").bitcast(FP8X4),
                scales=sender_scales[:, h, g, group].rearrange("p l r -> p (l r)"),
                in_=repeated[first, g][:],
            )

        def sender(j):
            return sender_codes[:, j // IL, :, j % IL, :], sender_scales[:, j // IL, :, j % IL, :]

        def multiply_nodes(h, name, rows, n, copy):
            bank = sum_psum.tile([P, BANK], F32, name="product", tag=("soft_bank", "gated_bank")[n])
            mx_group(bank[:], ((x_codes[:, h], x_scales[:, h], name),), n)
            copy(out=rows[:, n * BANK : (n + 1) * BANK], in_=bank[:])

        receiver_rows = [keep.tile([P, C], F32, name="receiver_rows_%d" % h) for h in range(HALVES)]
        own_rows = [keep.tile([P, C], F32, name="own_rows_%d" % h) for h in range(HALVES)]

        def park_senders():
            for h in range(HALVES):
                product = work.tile([P, C], F32, name="product", tag="agg", bufs=AGG_BUFS)
                for n in range(BANKS):
                    multiply_nodes(h, "WV", product, n, nc.scalar.copy)
                nc.sync.dma_start(out=x_out_rows[h], in_=product[:])

        sent = {}

        def fetch(j):
            sent[j] = rows_pool.tile([P, C], F32, name="sender", tag="node_rows", align_bytes=64)
            nc.sync.dma_start(out=sent[j][:], in_=out_0[:, j, :].unsqueeze(1).to_broadcast([GRAPHS, IL, C]))

        grouped = {}
        edge_codes = {}
        edge_scales = {}
        agg = {}
        sums = {}
        moments = {}
        mean = {}
        mean_sq = {}
        rstd = {}
        soft = {}
        gated = {}
        soft_banks = []
        gated_banks = []

        def flip(t):
            grouped[t] = work.tile([P, PASSES, P, PACK], BF16, name="grouped", align_bytes=64)
            flipped = flip_psum.tile([P, PASSES, PAIRS, P], F32, name="flipped")
            features_to_partitions(edge_sb[t][:], grouped[t], flipped)

        def quantise(t):
            edge_codes[t] = work.tile([P, PASSES, P], U32, name="edge_codes", bufs=3, align_bytes=64)
            edge_scales[t] = work.tile([P, PASSES, P], U8, name="edge_scales", bufs=3, align_bytes=64)
            nc.vector.quantize_mx(
                out=edge_codes[t][:].rearrange("p g r -> p (g r)").bitcast(FP8X4),
                scales=edge_scales[t][:].rearrange("p g r -> p (g r)"),
                in_=grouped[t][:].rearrange("p g r t -> p (g r t)"),
            )

        banks_in = {}

        def multiply(t, n):
            send_codes, send_scales = sender(t % NODES)
            acc = acc_psum.tile([P, BANK], F32, name="acc")
            mx_group(
                acc[:],
                ((edge_codes[t], edge_scales[t], "WE"), (send_codes, send_scales, "WB")),
                n,
            )
            banks_in[t, n] = acc

        def empty(t, n):
            if n == 0:
                agg[t] = work.tile([P, C], F32, name="agg", bufs=AGG_BUFS)
                sums[t] = small.tile([P, BANKS + 1], F32, name="sums")
            cols = slice(n * BANK, (n + 1) * BANK)
            nc.vector.scalar_tensor_tensor(
                out=agg[t][:, cols],
                in0=receiver_rows[t // NODES][:, cols],
                scalar=1.0,
                in1=banks_in[t, n][:],
                op0=ALU.mult,
                op1=ALU.add,
                accum_out=sums[t][:, n : n + 1],
            )

        def square(t):
            sum_of_squares(agg[t][:], sums[t][:, BANKS:])

        def take_moments(t):
            moments[t], mean[t], mean_sq[t] = moments_of(sums[t])

        def deviate(t):
            var_eps = variance_of(moments[t][:, BANKS:], mean_sq[t])
            rstd[t] = small.tile([P, 1], F32, name="rstd")
            nc.gpsimd.tensor_tensor(out=rstd[t][:], in0=var_eps[:], in1=minus_half[:], op=ALU.pow)

        WHOLE = (slice(0, C),)
        BY_BANK = tuple(slice(n * BANK, (n + 1) * BANK) for n in range(BANKS))

        def rectify(t):
            nc.vector.tensor_scalar(
                out=agg[t][:], in0=agg[t][:], scalar1=mean[t][:], scalar2=0.0, op0=ALU.subtract, op1=ALU.max
            )

        def add_residual(t, parts):
            h, j = divmod(t, NODES)
            for cols in parts:
                nc.vector.scalar_tensor_tensor(
                    out=agg[t][:, cols],
                    in0=agg[t][:, cols],
                    scalar=rstd[t][:],
                    in1=edge_sb[t][:, cols],
                    op0=ALU.mult,
                    op1=ALU.add,
                )
            nc.sync.dma_start(out=edge_out_rows[h, j], in_=agg[t][:])

        def squash(t, parts):
            soft[t] = work.tile([P, C], F32, name="soft", bufs=SOFT_BUFS)
            for cols in parts:
                nc.scalar.activation(out=soft[t][:, cols], in_=agg[t][:, cols], func=ACT.Tanh, scale=0.5)

        def exponentiate(t, parts):
            for cols in parts:
                nc.scalar.activation(out=soft[t][:, cols], in_=soft[t][:, cols], func=ACT.Exp, scale=0.5)

        def add_up(values, banks, j):
            for n in range(BANKS):
                for k in range(BLOCKS):
                    first = n * BANK + k * P
                    nc.tensor.matmul(
                        out=banks[n][:, k, :],
                        lhsT=values[:, first : first + P],
                        rhs=ident[:],
                        is_transpose=True,
                        start=(j == 0 and k == 0),
                        stop=(j == NODES - 1 and k == BLOCKS - 1),
                    )

        def open_banks(banks, name):
            banks.clear()
            for n in range(BANKS):
                bank = sum_psum.tile([P, BLOCKS, P], F32, name=name)
                banks.append(bank)

        def add_soft(t):
            if t % NODES == 0:
                open_banks(soft_banks, "soft_bank")
            add_up(soft[t], soft_banks, t % NODES)

        def gate(t, parts):
            gated[t] = work.tile([P, C], F32, name="gated", bufs=GATED_BUFS)
            for cols in parts:
                nc.vector.tensor_tensor(
                    out=gated[t][:, cols], in0=soft[t][:, cols], in1=sent[t % NODES][:, cols], op=ALU.mult
                )

        def add_gated(t):
            if t % NODES == 0:
                open_banks(gated_banks, "gated_bank")
            add_up(gated[t], gated_banks, t % NODES)

        soft_squared = {}
        gated_sum = {}

        def keep_soft(h):
            soft_squared[h] = keep.tile([P, C], F32, name="soft_squared_%d" % h)
            for n in range(BANKS):
                nc.scalar.activation(
                    out=soft_squared[h][:, n * BANK : (n + 1) * BANK],
                    in_=soft_banks[n][:].rearrange("p k r -> p (k r)"),
                    func=ACT.Square,
                    scale=float(NODES),
                )

        def keep_gated(h):
            gated_sum[h] = keep.tile([P, C], F32, name="gated_sum")
            for n in range(BANKS):
                cols = slice(n * BANK, (n + 1) * BANK)
                nc.vector.tensor_copy(out=gated_sum[h][:, cols], in_=gated_banks[n][:].rearrange("p k r -> p (k r)"))

        inverse = {}
        ratio = {}
        back = {}
        x_new = {}
        x_sums = {}
        x_mean = {}
        x_rstd = {}

        def invert(h):
            inverse[h] = work.tile([P, C], F32, name="inverse", tag="soft", bufs=SOFT_BUFS)
            for cols in BY_BANK:
                nc.scalar.activation(
                    out=inverse[h][:, cols], in_=soft_squared[h][:, cols], func=ACT.Abs_reciprocal_sqrt
                )

        def divide(h):
            ratio[h] = work.tile([P, C], F32, name="ratio", tag="gated", bufs=GATED_BUFS)
            for n, cols in enumerate(BY_BANK):
                gates = gated_sum[0][:, cols] if h == 0 else gated_banks[n][:].rearrange("p k r -> p (k r)")
                nc.vector.tensor_tensor(out=ratio[h][:, cols], in0=inverse[h][:, cols], in1=gates, op=ALU.mult)
                back[h, n] = acc_psum.tile([P, BANK], F32, name="back", tag="acc")
                for k in range(BLOCKS):
                    first = n * BANK + k * P
                    nc.tensor.transpose(
                        back[h, n][:, k * P : (k + 1) * P], ratio[h][:, first : first + P], ident[:]
                    )

        def renew(h):
            x_new[h] = work.tile([P, C], F32, name="x_new", tag="agg", bufs=AGG_BUFS)
            x_sums[h] = small.tile([P, 2 * BANKS], F32, name="x_sums")
            for n, cols in enumerate(BY_BANK):
                nc.vector.scalar_tensor_tensor(
                    out=x_new[h][:, cols],
                    in0=own_rows[h][:, cols],
                    scalar=1.0,
                    in1=back[h, n][:],
                    op0=ALU.mult,
                    op1=ALU.add,
                    accum_out=x_sums[h][:, n : n + 1],
                )

        def square_nodes(h):
            for n, cols in enumerate(BY_BANK):
                sum_of_squares(x_new[h][:, cols], x_sums[h][:, BANKS + n : BANKS + n + 1])

        def take_node_moments(h):
            bank = stat_psum.tile([P, 2 * BANKS], F32, name="node_bank", tag="moments")
            nc.tensor.matmul(out=bank[:], lhsT=group_mean[:], rhs=x_sums[h][:], start=True, stop=True)
            x_mean[h] = add_parts(bank[:, 0:BANKS], "x_mean")
            square_mean = add_parts(bank[:, BANKS:], "x_square_mean")
            mean_sq = small.tile([P, 1], F32, name="x_mean_sq")
            nc.scalar.activation(out=mean_sq[:], in_=x_mean[h][:], func=ACT.Square)
            var_eps = variance_of(square_mean[:], mean_sq)
            x_rstd[h] = small.tile([P, 1], F32, name="x_rstd")
            nc.scalar.activation(out=x_rstd[h][:], in_=var_eps[:], func=ACT.Abs_reciprocal_sqrt)

        def finish(h):
            shift = small.tile([P, 1], F32, name="shift")
            nc.vector.scalar_tensor_tensor(
                out=shift[:], in0=x_mean[h][:], scalar=-1.0, in1=x_rstd[h][:], op0=ALU.mult, op1=ALU.mult
            )
            for cols in BY_BANK:
                nc.vector.scalar_tensor_tensor(
                    out=x_new[h][:, cols],
                    in0=x_new[h][:, cols],
                    scalar=x_rstd[h][:],
                    in1=x_sb[:, h, cols],
                    op0=ALU.mult,
                    op1=ALU.add,
                )
                nc.scalar.activation(
                    out=x_new[h][:, cols], in_=x_new[h][:, cols], func=ACT.Relu, bias=shift[:]
                )
                nc.sync.dma_start(out=x_out_rows[h][:, :, cols], in_=x_new[h][:, cols])

        def due(t):
            return 0 <= t < TILES

        with tc.manual_schedule(
            engines={mybir.EngineType.PE, mybir.EngineType.Activation, mybir.EngineType.DVE}
        ):
            for h in range(HALVES):
                flipped = sum_psum.tile([P, PASSES, PAIRS, P], F32, name="nodes_flipped", tag="soft_bank")
                features_to_partitions(x_sb[:, h, :], x_grouped[:, h], flipped)
            for g in range(PASSES):
                repeat_senders(0, g, nc.vector.tensor_copy)
                quantise_senders(0, g)
            flip(0)
            warm = stat_psum.tile([P, P], F32, name="warm", tag="moments")
            for k in range(WARM_UP):
                nc.tensor.transpose(warm[:], ident[:], ident[:])
            quantise_nodes()
            quantise(0)
            for g in range(PASSES):
                repeat_senders(SENDERS, g, nc.scalar.copy)
                quantise_senders(SENDERS, g)
            multiply_nodes(0, "WA", receiver_rows[0], 0, nc.scalar.copy)
            last = TILES - 1
            for r in range(TILES):
                multiply(r, 0)
                if r == 0:
                    flip(1)
                    multiply_nodes(0, "WA", receiver_rows[0], 1, nc.scalar.copy)
                empty(r, 0)
                if due(r + 1):
                    quantise(r + 1)
                multiply(r, 1)
                empty(r, 1)
                if due(r - 1):
                    take_moments(r - 1)
                if r == last:
                    rectify(r - 1)
                    deviate(r - 1)
                square(r)
                if due(r + 2):
                    flip(r + 2)
                if r == 0:
                    for n in range(BANKS):
                        multiply_nodes(1, "WA", receiver_rows[1], n, nc.scalar.copy)
                if r == 1:
                    park_senders()
                if due(r - 3):
                    exponentiate(r - 3, WHOLE)
                if due(r - 4):
                    gate(r - 4, WHOLE)
                if due(r - 2):
                    add_residual(r - 2, WHOLE)
                    squash(r - 2, WHOLE)
                if r == 2:
                    for h in range(HALVES):
                        for n in range(BANKS):
                            multiply_nodes(h, "WU", own_rows[h], n, nc.vector.tensor_copy)
                if due(r - 1) and r < last:
                    rectify(r - 1)
                    deviate(r - 1)
                if due(r - 5):
                    add_soft(r - 5)
                    add_gated(r - 5)
                if r - 5 == NODES - 1:
                    keep_soft(0)
                    keep_gated(0)
                if r < HALVES:
                    for g in range(PASSES):
                        repeat_senders(IL + r * SENDERS, g, nc.vector.tensor_copy)
                        quantise_senders(IL + r * SENDERS, g)
                if r == 1:
                    fetch(0)
                    fetch(1)
                if 1 <= r < NODES - 1:
                    fetch(r + 1)
                if due(r + LOAD_AHEAD):
                    load(r + LOAD_AHEAD)

            take_moments(last)
            add_residual(last - 1, WHOLE)
            squash(last - 1, WHOLE)
            rectify(last)
            deviate(last)
            exponentiate(last - 2, WHOLE)
            gate(last - 3, WHOLE)
            add_residual(last, BY_BANK)
            exponentiate(last - 1, WHOLE)
            squash(last, BY_BANK)
            gate(last - 2, WHOLE)
            exponentiate(last, BY_BANK)
            for t in (last - 4, last - 3, last - 2):
                add_soft(t)
                add_gated(t)
            gate(last - 1, WHOLE)
            gate(last, BY_BANK)
            for t in (last - 1, last):
                add_soft(t)
                add_gated(t)
            invert(0)
            keep_soft(1)
            invert(1)
            divide(0)
            renew(0)
            divide(1)
            renew(1)
            square_nodes(0)
            take_node_moments(0)
            square_nodes(1)
            finish(0)
            take_node_moments(1)
            finish(1)
